import numpy as np
import ml_dtypes


def mxq(x, axis, fmt="e4m3"):
    dtype, down = {"e4m3": (ml_dtypes.float8_e4m3fn, 7), "e5m2": (ml_dtypes.float8_e5m2, 14)}[fmt]
    v = np.moveaxis(np.asarray(x, np.float32).astype(ml_dtypes.bfloat16).astype(np.float64), axis, -1)
    blocks = v.reshape(v.shape[:-1] + (-1, 32))
    amax = np.abs(blocks).max(-1, keepdims=True)
    byte = np.maximum(np.where(amax > 0, np.frexp(amax)[1] - 1 + 127, 0) - down, 1)
    scale = np.exp2(byte - 127.0)
    codes = (blocks / scale).astype(np.float32).astype(dtype).astype(np.float64)
    return np.moveaxis((codes * scale).reshape(v.shape), -1, axis)


WIDE = False


def mx_kscale(k):
    if not WIDE:
        return np.ones(k)
    levels = np.array([10, -10, 5, -5, 0])
    a = np.random.permutation(np.resize(levels, k // 512 * 4)).reshape(k // 512, 4)
    idx = np.arange(k)
    return np.exp2(a[idx // 512, idx % 128 // 32])


BF16 = ml_dtypes.bfloat16


def bf(x):
    return np.asarray(x, np.float32).astype(BF16)


def f64(x):
    return np.asarray(x).astype(np.float64)


E2M1 = np.array([0.0, 0.5, 1.0, 1.5, 2.0, 3.0, 4.0, 6.0, -0.0, -0.5, -1.0, -1.5, -2.0, -3.0, -4.0, -6.0])


def pack_weight(w, fmt):
    k, n = w.shape
    w = f64(bf(w)).reshape(k // 32, 32, n)
    amax = np.abs(w).max(1)
    if fmt == "e4m3":
        byte = np.frexp(amax)[1] - 1 + 127 - 7
    else:
        mant, ex = np.frexp(amax / 6.0)
        byte = np.where(mant > 0.5, ex, ex - 1) + 127
    byte = np.clip(np.where(amax > 0, byte, 1), 1, 254)
    scaled = (w * np.exp2(127.0 - byte)[:, None, :]).reshape(k, n).astype(np.float32)
    by_word = np.ascontiguousarray(scaled.reshape(k // 512, 128, 4, n).transpose(0, 1, 3, 2))
    if fmt == "e4m3":
        words = by_word.astype(ml_dtypes.float8_e4m3fn).view(np.uint8)
    else:
        c = by_word.astype(ml_dtypes.float4_e2m1fn).view(np.uint8) & 0xF
        words = c[..., 0::2] | (c[..., 1::2] << 4)
    return np.ascontiguousarray(words), np.ascontiguousarray(byte.astype(np.uint8).reshape(k // 512, 16, n))


def unpack_weight(words, scales, fmt):
    g, p, n, _ = words.shape
    if fmt == "e4m3":
        vals = np.ascontiguousarray(words).view(ml_dtypes.float8_e4m3fn).astype(np.float64)
    else:
        nib = np.empty((g, p, n, 4), np.uint8)
        nib[..., 0::2] = words & 0xF
        nib[..., 1::2] = words >> 4
        vals = E2M1[nib]
    vals = vals * np.repeat(np.exp2(scales.astype(np.float64) - 127.0), 8, axis=1)[..., None]
    return vals.transpose(0, 1, 3, 2).reshape(g * 512, n)


B, F, C, H = 2, 64, 3072, 1024
K = C + H
FMT = "e4m3"


def sigmoid(v):
    return 1.0 / (1.0 + np.exp(-v))


def setup_inputs():
    s = mx_kscale(K)

    def w():
        return pack_weight(np.ascontiguousarray((np.random.standard_normal((H, K)) / np.sqrt(K) / s[None, :]).T), FMT)

    def b():
        return bf(np.random.standard_normal(H) * 0.3)

    x = bf(np.random.standard_normal((B, F, C)) * s[None, None, :C])
    hidden_state = bf(np.random.standard_normal((B, H, F)) * s[None, C:, None])
    cell_state = bf(np.random.standard_normal((B, H, F)))
    W_f_words, W_f_scales = w()
    b_f = b()
    W_i_words, W_i_scales = w()
    b_i = b()
    W_o_words, W_o_scales = w()
    b_o = b()
    W_g_words, W_g_scales = w()
    b_g = b()
    return {"x": x,
            "hidden_state": hidden_state,
            "cell_state": cell_state,
            "W_f_words": W_f_words, "W_f_scales": W_f_scales, "b_f": b_f,
            "W_i_words": W_i_words, "W_i_scales": W_i_scales, "b_i": b_i,
            "W_o_words": W_o_words, "W_o_scales": W_o_scales, "b_o": b_o,
            "W_g_words": W_g_words, "W_g_scales": W_g_scales, "b_g": b_g}


def reference(x, hidden_state, cell_state, W_f_words, W_f_scales, b_f, W_i_words, W_i_scales, b_i, W_o_words, W_o_scales, b_o, W_g_words, W_g_scales, b_g):
    xh = np.concatenate([np.swapaxes(f64(x), 1, 2), f64(hidden_state)], axis=1)
    W = np.concatenate([unpack_weight(W_f_words, W_f_scales, FMT).T,
                        unpack_weight(W_i_words, W_i_scales, FMT).T,
                        unpack_weight(W_g_words, W_g_scales, FMT).T,
                        unpack_weight(W_o_words, W_o_scales, FMT).T], axis=0)
    b = np.concatenate([f64(b_f), f64(b_i), f64(b_g), f64(b_o)], axis=0)
    gates = (W @ mxq(xh, 1, "e4m3")) + b[None, :, None]
    f_t = sigmoid(gates[:, 0 * H:1 * H])
    i_t = sigmoid(gates[:, 1 * H:2 * H])
    g_t = np.tanh(gates[:, 2 * H:3 * H])
    o_t = sigmoid(gates[:, 3 * H:4 * H])
    new_cell = f64(cell_state) * f_t + i_t * g_t
    new_hidden = np.tanh(new_cell) * o_t
    return (np.swapaxes(new_hidden, 1, 2), new_hidden, new_cell)

@@ -1,0 +1,199 @@
+from contextlib import ExitStack
+
+import concourse.mybir as mybir
+from concourse.masks import make_identity
+
+F32 = mybir.dt.float32
+BF16 = mybir.dt.bfloat16
+I32 = mybir.dt.int32
+U32 = mybir.dt.uint32
+U8 = mybir.dt.uint8
+FP8X4 = mybir.dt.float8_e4m3fn_x4
+ACT = mybir.ActivationFunctionType
+ALU = mybir.AluOpType
+
+P = 128
+B, F, C, H = 2, 64, 3072, 1024
+K = C + H
+G = K // 512
+GX = C // 512
+NCH = H // P
+FLOPS = 2 * 4 * H * K * B * F
+
+O_PIECES = [
+    (0, 6, [[0, 1], [2, 3], [4, 5], [6, 7]]),
+    (6, 8, [[0, 1, 2, 3], [4, 5, 6, 7]]),
+]
+
+
+def tile_batchedlstm_w_kernel(
+    tc, x, hidden_state, cell_state,
+    W_f_words, W_f_scales, b_f,
+    W_i_words, W_i_scales, b_i,
+    W_o_words, W_o_scales, b_o,
+    W_g_words, W_g_scales, b_g,
+    out_0, out_1, out_2,
+):
+    nc = tc.nc
+    words = [W_f_words, W_i_words, W_g_words, W_o_words]
+    scales = [W_f_scales, W_i_scales, W_g_scales, W_o_scales]
+    biases = [b_f, b_i, b_g, b_o]
+    funcs = [ACT.Sigmoid, ACT.Sigmoid, ACT.Tanh, ACT.Sigmoid]
+
+    with ExitStack() as ctx:
+        keep = ctx.enter_context(tc.tile_pool(name="keep", bufs=1))
+        psum = ctx.enter_context(tc.psum_pool(name="psum", bufs=1))
+
+        w_sb = [keep.tile([P, G, H], U32, name="w%d" % gi, align_bytes=64) for gi in range(4)]
+        planes = keep.tile([P, 4, 2, H], U8, name="planes", align_bytes=64)
+        x_sb = keep.tile([P, C], BF16, name="x_sb", align_bytes=64)
+        h_raw = keep.tile([P, 2, B, 4 * F], BF16, name="h_raw", align_bytes=64)
+        grouped = keep.tile([P, G, P, 4], BF16, name="grouped", align_bytes=64)
+        xh_codes = keep.tile([P, G, P], U32, name="xh_codes", align_bytes=64)
+        xh_scales = keep.tile([P, G, P], U8, name="xh_scales", align_bytes=64)
+        ident = keep.tile([P, P], F32, name="ident")
+        b_raw = keep.tile([P, P], BF16, name="b_raw")
+        b_f32 = keep.tile([P, P], F32, name="b_f32")
+        bias_sb = keep.tile([P, 32], F32, name="bias_sb")
+        c_sb = keep.tile([P, NCH, P], BF16, name="c_sb")
+        gate_sb = [keep.tile([P, NCH, P], F32, name="gate%d" % gi) for gi in range(4)]
+        nc_sb = keep.tile([P, NCH, P], F32, name="nc_sb")
+        th_sb = keep.tile([P, NCH, P], F32, name="th_sb")
+        nh_sb = keep.tile([P, NCH, P], F32, name="nh_sb")
+        o0_sb = keep.tile([P, NCH, P], F32, name="o0_sb")
+        bank = [psum.tile([P, 4, P], F32, name="bank%d" % j) for j in range(8)]
+
+        nc.vector.memset(planes[:].rearrange("p a b n -> p (a b n)").bitcast(I32), 0)
+        nc.vector.memset(b_raw[:], 0.0)
+        make_identity(nc, ident[:])
+
+        nc.sync.dma_start(out=x_sb[:], in_=x.rearrange("b f c -> (b f) c"))
+        for gi in range(4):
+            nc.sync.dma_start(out=b_raw[8 * gi:8 * gi + 8, :],
+                              in_=biases[gi].rearrange("(c p) -> c p", p=P))
+        for b in range(B):
+            nc.sync.dma_start(
+                out=h_raw[:, :, b, :],
+                in_=hidden_state[b].rearrange("(g p t) f -> p g (t f)", g=2, p=P, t=4))
+
+        def load_scales(gi, eng, view):
+            for gh in range(2):
+                for q in range(4):
+                    eng.dma_start(
+                        out=planes[32 * q:32 * q + 16, gi, gh, :].bitcast(view),
+                        in_=scales[gi][4 * gh:4 * gh + 4, 4 * q:4 * q + 4, :].bitcast(view))
+
+        load_scales(0, nc.sync, I32)
+        for gi in range(1, 4):
+            load_scales(gi, nc.gpsimd, F32)
+
+        def load_words(gi, g0, g1, c0, c1):
+            nc.sync.dma_start(
+                out=w_sb[gi][:, g0:g1, c0 * P:c1 * P].bitcast(I32),
+                in_=words[gi][g0:g1].rearrange("g p n t -> p g (n t)")[:, :, c0 * 4 * P:c1 * 4 * P].bitcast(I32))
+
+        for g in range(G):
+            load_words(0, g, g + 1, 0, NCH)
+        for b in range(B):
+            nc.sync.dma_start(
+                out=c_sb[:, :, b * F:(b + 1) * F],
+                in_=cell_state[b].rearrange("(c p) f -> p c f", p=P))
+        for gi in (1, 2):
+            for g in range(G):
+                load_words(gi, g, g + 1, 0, NCH)
+        for c0, c1, gsplits in O_PIECES:
+            for gs in gsplits:
+                load_words(3, gs[0], gs[-1] + 1, c0, c1)
+
+        x_words = x_sb[:].bitcast(F32)
+        for g in range(GX):
+            for u in range(2):
+                nc.tensor.transpose(bank[g // 2][:, (g % 2) * 2 + u, :],
+                                    x_words[:, 256 * g + u:256 * (g + 1):2], ident[:])
+        nc.vector.tensor_copy(out=b_f32[:], in_=b_raw[:])
+        nc.tensor.transpose(bank[3][:, 0, :], b_f32[:], ident[:])
+
+        grouped_w = grouped[:].bitcast(F32)
+        nc.vector.tensor_copy(
+            out=grouped[:, GX:G, :, :].rearrange("p g (b f) t -> p (g b) f t", b=B),
+            in_=h_raw[:].rearrange("p g b (t f) -> p (g b) f t", t=4))
+        for j in range(GX // 2):
+            src = bank[j][:].rearrange("p (g u) c -> p g c u", u=2)
+            dst = grouped_w[:, 2 * j:2 * j + 2, :, :]
+            if j == 1:
+                nc.scalar.copy(out=dst, in_=src)
+            else:
+                nc.vector.tensor_copy(out=dst, in_=src)
+        nc.vector.tensor_copy(out=bias_sb[:], in_=bank[3][:, 0, 0:32])
+        for half in range(2):
+            gs = slice(4 * half, 4 * half + 4)
+            nc.vector.quantize_mx(
+                out=xh_codes[:, gs, :].rearrange("p g c -> p (g c)").bitcast(FP8X4),
+                scales=xh_scales[:, gs, :].rearrange("p g c -> p (g c)"),
+                in_=grouped[:, gs, :, :].rearrange("p g c t -> p (g c t)"))
+
+        def passes(gi, g, chunks):
+            k = 4 * (g % 4)
+            for hc in chunks:
+                cols = slice(hc * P, (hc + 1) * P)
+                nc.tensor.matmul_mx(
+                    out=bank[hc][:, gi, :],
+                    lhsT=w_sb[gi][:, g, cols].bitcast(FP8X4),
+                    lhsT_scale=planes[k:P, gi, g // 4, cols],
+                    rhs=xh_codes[:, g, :].bitcast(FP8X4),
+                    rhs_scale=xh_scales[:, g, :],
+                    start=(g == 0), stop=(g == G - 1))
+
+        def activate(gi, chunks):
+            for hc in chunks:
+                nc.scalar.activation(
+                    out=gate_sb[gi][:, hc, :], in_=bank[hc][:, gi, :], func=funcs[gi],
+                    bias=bias_sb[:, 8 * gi + hc:8 * gi + hc + 1], scale=1.0)
+
+        allc = list(range(NCH))
+        for g in range(G):
+            passes(0, g, allc)
+        activate(0, allc)
+        nc.vector.tensor_tensor(out=gate_sb[0][:], in0=gate_sb[0][:], in1=c_sb[:], op=ALU.mult)
+        for g in range(G):
+            passes(1, g, allc)
+        activate(1, allc)
+        for g in range(G):
+            passes(2, g, allc)
+        for half in range(2):
+            hs = slice(4 * half, 4 * half + 4)
+            activate(2, allc[hs])
+            nc.vector.tensor_tensor(out=gate_sb[1][:, hs, :], in0=gate_sb[1][:, hs, :],
+                                    in1=gate_sb[2][:, hs, :], op=ALU.mult)
+            nc.vector.tensor_tensor(out=nc_sb[:, hs, :], in0=gate_sb[0][:, hs, :],
+                                    in1=gate_sb[1][:, hs, :], op=ALU.add)
+            nc.scalar.activation(out=th_sb[:, hs, :], in_=nc_sb[:, hs, :], func=ACT.Tanh)
+        for b in range(B):
+            nc.sync.dma_start(out=out_2[b].rearrange("(c p) f -> p c f", p=P),
+                              in_=nc_sb[:, :, b * F:(b + 1) * F])
+
+        out_0_rows = out_0.rearrange("b f h -> (b f) h")
+        for c0, c1, gsplits in O_PIECES:
+            chunks = allc[c0:c1]
+            for gs in gsplits:
+                for g in gs:
+                    passes(3, g, chunks)
+            activate(3, chunks)
+            nc.vector.tensor_tensor(out=nh_sb[:, c0:c1, :], in0=th_sb[:, c0:c1, :],
+                                    in1=gate_sb[3][:, c0:c1, :], op=ALU.mult)
+            for b in range(B):
+                nc.sync.dma_start(
+                    out=out_1[b].rearrange("(c p) f -> p c f", p=P)[:, c0:c1, :],
+                    in_=nh_sb[:, c0:c1, b * F:(b + 1) * F])
+            for j, hc in enumerate(chunks):
+                nc.tensor.transpose(bank[chunks[j // 4]][:, j % 4, :], nh_sb[:, hc, :], ident[:])
+            for j0 in range(0, len(chunks), 4):
+                n = min(4, len(chunks) - j0)
+                dst = o0_sb[:, c0 + j0:c0 + j0 + n, :]
+                src = bank[chunks[j0 // 4]][:, 0:n, :]
+                if (j0 // 4) % 2 == 0:
+                    nc.vector.tensor_copy(out=dst, in_=src)
+                else:
+                    nc.scalar.copy(out=dst, in_=src)
+            nc.sync.dma_start(out=out_0_rows[:, c0 * P:c1 * P],
+                              in_=o0_sb[:, c0:c1, :].rearrange("p c m -> p (c m)"))

@@ -19,11 +19,8 @@ G = K // 512
 GX = C // 512
 NCH = H // P
 FLOPS = 2 * 4 * H * K * B * F
-
-O_PIECES = [
-    (0, 6, [[0, 1], [2, 3], [4, 5], [6, 7]]),
-    (6, 8, [[0, 1, 2, 3], [4, 5, 6, 7]]),
-]
+LAST_SPLIT = 4
+SCALES_ON_SYNC = []
 
 
 def tile_batchedlstm_w_kernel(
@@ -43,6 +40,7 @@ def tile_batchedlstm_w_kernel(
     with ExitStack() as ctx:
         keep = ctx.enter_context(tc.tile_pool(name="keep", bufs=1))
         psum = ctx.enter_context(tc.psum_pool(name="psum", bufs=1))
+        ctx.enter_context(tc.manual_schedule())
 
         w_sb = [keep.tile([P, G, H], U32, name="w%d" % gi, align_bytes=64) for gi in range(4)]
         planes = keep.tile([P, 4, 2, H], U8, name="planes", align_bytes=64)
@@ -67,70 +65,77 @@ def tile_batchedlstm_w_kernel(
         nc.vector.memset(b_raw[:], 0.0)
         make_identity(nc, ident[:])
 
+        def load_scales(gi):
+            for gh in range(2):
+                for q in range(4):
+                    dst = planes[32 * q:32 * q + 16, gi, gh, :]
+                    src = scales[gi][4 * gh:4 * gh + 4, 4 * q:4 * q + 4, :]
+                    if gi in SCALES_ON_SYNC:
+                        nc.sync.dma_start(out=dst.bitcast(I32), in_=src.bitcast(I32))
+                    else:
+                        nc.gpsimd.dma_start(out=dst.bitcast(F32), in_=src.bitcast(F32))
+
+        def load_words(gi, g0, g1, n0, n1):
+            nc.sync.dma_start(
+                out=w_sb[gi][:, g0:g1, n0:n1].bitcast(I32),
+                in_=words[gi][g0:g1].rearrange("g p n t -> p g (n t)")[:, :, 4 * n0:4 * n1].bitcast(I32))
+
         nc.sync.dma_start(out=x_sb[:], in_=x.rearrange("b f c -> (b f) c"))
         for gi in range(4):
             nc.sync.dma_start(out=b_raw[8 * gi:8 * gi + 8, :],
                               in_=biases[gi].rearrange("(c p) -> c p", p=P))
+        for gi in range(4):
+            load_scales(gi)
+        for g in range(3):
+            load_words(0, g, g + 1, 0, H)
         for b in range(B):
             nc.sync.dma_start(
                 out=h_raw[:, :, b, :],
                 in_=hidden_state[b].rearrange("(g p t) f -> p g (t f)", g=2, p=P, t=4))
-
-        def load_scales(gi, eng, view):
-            for gh in range(2):
-                for q in range(4):
-                    eng.dma_start(
-                        out=planes[32 * q:32 * q + 16, gi, gh, :].bitcast(view),
-                        in_=scales[gi][4 * gh:4 * gh + 4, 4 * q:4 * q + 4, :].bitcast(view))
-
-        load_scales(0, nc.sync, I32)
-        for gi in range(1, 4):
-            load_scales(gi, nc.gpsimd, F32)
-
-        def load_words(gi, g0, g1, c0, c1):
-            nc.sync.dma_start(
-                out=w_sb[gi][:, g0:g1, c0 * P:c1 * P].bitcast(I32),
-                in_=words[gi][g0:g1].rearrange("g p n t -> p g (n t)")[:, :, c0 * 4 * P:c1 * 4 * P].bitcast(I32))
-
-        for g in range(G):
-            load_words(0, g, g + 1, 0, NCH)
+        for g in range(3, G):
+            load_words(0, g, g + 1, 0, H)
         for b in range(B):
             nc.sync.dma_start(
                 out=c_sb[:, :, b * F:(b + 1) * F],
                 in_=cell_state[b].rearrange("(c p) f -> p c f", p=P))
         for gi in (1, 2):
             for g in range(G):
-                load_words(gi, g, g + 1, 0, NCH)
-        for c0, c1, gsplits in O_PIECES:
-            for gs in gsplits:
-                load_words(3, gs[0], gs[-1] + 1, c0, c1)
+                load_words(gi, g, g + 1, 0, H)
+        for g in range(G - 1):
+            load_words(3, g, g + 1, 0, H)
+        for s in range(LAST_SPLIT):
+            w = H // LAST_SPLIT
+            load_words(3, G - 1, G, s * w, (s + 1) * w)
 
         x_words = x_sb[:].bitcast(F32)
         for g in range(GX):
             for u in range(2):
                 nc.tensor.transpose(bank[g // 2][:, (g % 2) * 2 + u, :],
                                     x_words[:, 256 * g + u:256 * (g + 1):2], ident[:])
-        nc.vector.tensor_copy(out=b_f32[:], in_=b_raw[:])
-        nc.tensor.transpose(bank[3][:, 0, :], b_f32[:], ident[:])
 
         grouped_w = grouped[:].bitcast(F32)
-        nc.vector.tensor_copy(
-            out=grouped[:, GX:G, :, :].rearrange("p g (b f) t -> p (g b) f t", b=B),
-            in_=h_raw[:].rearrange("p g b (t f) -> p (g b) f t", t=4))
-        for j in range(GX // 2):
-            src = bank[j][:].rearrange("p (g u) c -> p g c u", u=2)
-            dst = grouped_w[:, 2 * j:2 * j + 2, :, :]
-            if j == 1:
-                nc.scalar.copy(out=dst, in_=src)
-            else:
-                nc.vector.tensor_copy(out=dst, in_=src)
-        nc.vector.tensor_copy(out=bias_sb[:], in_=bank[3][:, 0, 0:32])
-        for half in range(2):
+
+        def x_src(j):
+            return bank[j][:].rearrange("p (g u) c -> p g c u", u=2)
+
+        def quantise(half):
             gs = slice(4 * half, 4 * half + 4)
             nc.vector.quantize_mx(
                 out=xh_codes[:, gs, :].rearrange("p g c -> p (g c)").bitcast(FP8X4),
                 scales=xh_scales[:, gs, :].rearrange("p g c -> p (g c)"),
                 in_=grouped[:, gs, :, :].rearrange("p g c t -> p (g c t)"))
+
+        nc.vector.tensor_copy(out=grouped_w[:, 0:2, :, :], in_=x_src(0))
+        nc.scalar.copy(out=grouped_w[:, 2:4, :, :], in_=x_src(1))
+        nc.vector.tensor_copy(out=grouped_w[:, 4:6, :, :], in_=x_src(2))
+        nc.vector.tensor_copy(out=b_f32[:], in_=b_raw[:])
+        nc.tensor.transpose(bank[3][:, 0, :], b_f32[:], ident[:])
+        quantise(0)
+        nc.vector.tensor_copy(out=bias_sb[:], in_=bank[3][:, 0, 0:32])
+        nc.vector.tensor_copy(
+            out=grouped[:, GX:G, :, :].rearrange("p g (b f) t -> p (g b) f t", b=B),
+            in_=h_raw[:].rearrange("p g b (t f) -> p (g b) f t", t=4))
+        quantise(1)
 
         def passes(gi, g, chunks):
             k = 4 * (g % 4)
@@ -160,9 +165,9 @@ def tile_batchedlstm_w_kernel(
         activate(1, allc)
         for g in range(G):
             passes(2, g, allc)
+        activate(2, allc)
         for half in range(2):
             hs = slice(4 * half, 4 * half + 4)
-            activate(2, allc[hs])
             nc.vector.tensor_tensor(out=gate_sb[1][:, hs, :], in0=gate_sb[1][:, hs, :],
                                     in1=gate_sb[2][:, hs, :], op=ALU.mult)
             nc.vector.tensor_tensor(out=nc_sb[:, hs, :], in0=gate_sb[0][:, hs, :],
@@ -172,28 +177,34 @@ def tile_batchedlstm_w_kernel(
             nc.sync.dma_start(out=out_2[b].rearrange("(c p) f -> p c f", p=P),
                               in_=nc_sb[:, :, b * F:(b + 1) * F])
 
+        for g in range(G):
+            passes(3, g, allc)
+        activate(3, allc)
+
         out_0_rows = out_0.rearrange("b f h -> (b f) h")
-        for c0, c1, gsplits in O_PIECES:
-            chunks = allc[c0:c1]
-            for gs in gsplits:
-                for g in gs:
-                    passes(3, g, chunks)
-            activate(3, chunks)
-            nc.vector.tensor_tensor(out=nh_sb[:, c0:c1, :], in0=th_sb[:, c0:c1, :],
-                                    in1=gate_sb[3][:, c0:c1, :], op=ALU.mult)
+
+        def product(j):
+            cs = slice(2 * j, 2 * j + 2)
+            nc.vector.tensor_tensor(out=nh_sb[:, cs, :], in0=th_sb[:, cs, :],
+                                    in1=gate_sb[3][:, cs, :], op=ALU.mult)
             for b in range(B):
                 nc.sync.dma_start(
-                    out=out_1[b].rearrange("(c p) f -> p c f", p=P)[:, c0:c1, :],
-                    in_=nh_sb[:, c0:c1, b * F:(b + 1) * F])
-            for j, hc in enumerate(chunks):
-                nc.tensor.transpose(bank[chunks[j // 4]][:, j % 4, :], nh_sb[:, hc, :], ident[:])
-            for j0 in range(0, len(chunks), 4):
-                n = min(4, len(chunks) - j0)
-                dst = o0_sb[:, c0 + j0:c0 + j0 + n, :]
-                src = bank[chunks[j0 // 4]][:, 0:n, :]
-                if (j0 // 4) % 2 == 0:
-                    nc.vector.tensor_copy(out=dst, in_=src)
-                else:
-                    nc.scalar.copy(out=dst, in_=src)
-            nc.sync.dma_start(out=out_0_rows[:, c0 * P:c1 * P],
-                              in_=o0_sb[:, c0:c1, :].rearrange("p c m -> p (c m)"))
+                    out=out_1[b].rearrange("(c p) f -> p c f", p=P)[:, cs, :],
+                    in_=nh_sb[:, cs, b * F:(b + 1) * F])
+            for u in range(2):
+                nc.tensor.transpose(bank[2 * j][:, u, :], nh_sb[:, 2 * j + u, :], ident[:])
+
+        def leave(j, eng_copy):
+            cs = slice(2 * j, 2 * j + 2)
+            eng_copy(out=o0_sb[:, cs, :], in_=bank[2 * j][:, 0:2, :])
+            nc.sync.dma_start(out=out_0_rows[:, 2 * j * P:(2 * j + 2) * P],
+                              in_=o0_sb[:, cs, :].rearrange("p c m -> p (c m)"))
+
+        product(0)
+        product(1)
+        leave(0, nc.vector.tensor_copy)
+        product(2)
+        leave(1, nc.vector.tensor_copy)
+        product(3)
+        leave(2, nc.scalar.copy)
+        leave(3, nc.scalar.copy)

@@ -17,9 +17,9 @@ B, F, C, H = 2, 64, 3072, 1024
 K = C + H
 G = K // 512
 GX = C // 512
-NCH = H // P
+HALF = 512
+L = HALF // P
 FLOPS = 2 * 4 * H * K * B * F
-LAST_SPLIT = 4
 SCALES_ON_SYNC = []
 
 
@@ -50,19 +50,30 @@ def tile_batchedlstm_w_kernel(
         xh_codes = keep.tile([P, G, P], U32, name="xh_codes", align_bytes=64)
         xh_scales = keep.tile([P, G, P], U8, name="xh_scales", align_bytes=64)
         ident = keep.tile([P, P], F32, name="ident")
-        b_raw = keep.tile([P, P], BF16, name="b_raw")
-        b_f32 = keep.tile([P, P], F32, name="b_f32")
-        bias_sb = keep.tile([P, 32], F32, name="bias_sb")
-        c_sb = keep.tile([P, NCH, P], BF16, name="c_sb")
-        gate_sb = [keep.tile([P, NCH, P], F32, name="gate%d" % gi) for gi in range(4)]
-        nc_sb = keep.tile([P, NCH, P], F32, name="nc_sb")
-        th_sb = keep.tile([P, NCH, P], F32, name="th_sb")
-        nh_sb = keep.tile([P, NCH, P], F32, name="nh_sb")
-        o0_sb = keep.tile([P, NCH, P], F32, name="o0_sb")
-        bank = [psum.tile([P, 4, P], F32, name="bank%d" % j) for j in range(8)]
+        ones = keep.tile([P, P], BF16, name="ones")
+        b_row = keep.tile([P, 4, H], BF16, name="b_row")
+        bias_bc = keep.tile([P, 4, 2, L, P], F32, name="bias_bc")
+        c_raw = keep.tile([P, B * 2, L * F], BF16, name="c_raw")
+        c_f32 = keep.tile([P, 2, L, P], F32, name="c_f32")
+        gate_sb = [keep.tile([P, 2, L, P], F32, name="gate%d" % gi) for gi in range(4)]
+        z_cell = keep.tile([P, 2, B, L, F], F32, name="z_cell")
+        z_hid = keep.tile([P, 2, B, L, F], F32, name="z_hid")
+        z_tanh = keep.tile([P, 2, B, L, F], F32, name="z_tanh")
+        acc = [psum.tile([P, HALF], F32, name="acc%d" % j) for j in range(4)]
+        tmp = [psum.tile([P, HALF], F32, name="tmp%d" % j) for j in range(4)]
+
+        def slots(bank):
+            return bank[:].rearrange("p (a c) -> p a c", a=4)
+
+        def permuted(bank):
+            return bank[:].rearrange("p (hh l) -> p l hh", l=L)
+
+        def natural_view(t, hf):
+            return t[:, hf, :, :].rearrange("p l hh -> p (l hh)").rearrange("p (hh l) -> p hh l", l=L)
 
         nc.vector.memset(planes[:].rearrange("p a b n -> p (a b n)").bitcast(I32), 0)
-        nc.vector.memset(b_raw[:], 0.0)
+        nc.vector.memset(b_row[:].rearrange("p a n -> p (a n)").bitcast(I32), 0)
+        nc.vector.memset(ones[:], 1.0)
         make_identity(nc, ident[:])
 
         def load_scales(gi):
@@ -82,8 +93,8 @@ def tile_batchedlstm_w_kernel(
 
         nc.sync.dma_start(out=x_sb[:], in_=x.rearrange("b f c -> (b f) c"))
         for gi in range(4):
-            nc.sync.dma_start(out=b_raw[8 * gi:8 * gi + 8, :],
-                              in_=biases[gi].rearrange("(c p) -> c p", p=P))
+            nc.sync.dma_start(out=b_row[0:1, gi, :],
+                              in_=biases[gi].rearrange("(o n) -> o n", o=1))
         for gi in range(4):
             load_scales(gi)
         for g in range(3):
@@ -92,31 +103,66 @@ def tile_batchedlstm_w_kernel(
             nc.sync.dma_start(
                 out=h_raw[:, :, b, :],
                 in_=hidden_state[b].rearrange("(g p t) f -> p g (t f)", g=2, p=P, t=4))
+        nc.sync.dma_start(
+            out=c_raw[:],
+            in_=cell_state.rearrange("b (hf hh l) f -> hh (b hf) (l f)", hf=2, hh=P, l=L))
         for g in range(3, G):
             load_words(0, g, g + 1, 0, H)
-        for b in range(B):
-            nc.sync.dma_start(
-                out=c_sb[:, :, b * F:(b + 1) * F],
-                in_=cell_state[b].rearrange("(c p) f -> p c f", p=P))
         for gi in (1, 2):
             for g in range(G):
                 load_words(gi, g, g + 1, 0, H)
         for g in range(G - 1):
             load_words(3, g, g + 1, 0, H)
-        for s in range(LAST_SPLIT):
-            w = H // LAST_SPLIT
-            load_words(3, G - 1, G, s * w, (s + 1) * w)
+        for hf in range(2):
+            load_words(3, G - 1, G, hf * HALF, (hf + 1) * HALF)
+
+        def bias_unit(gi, hf, bank, copy):
+            nc.tensor.matmul(out=bank[:], lhsT=ones[:], rhs=b_row[:, gi, hf * HALF:(hf + 1) * HALF],
+                             start=True, stop=True)
+            copy(out=bias_bc[:, gi, hf, :, :], in_=permuted(bank))
+
+        def passes(gi, g, banks, halves):
+            k = 4 * (g % 4)
+            for hf in halves:
+                cols = slice(hf * HALF, (hf + 1) * HALF)
+                nc.tensor.matmul_mx(
+                    out=banks[hf][:],
+                    lhsT=xh_codes[:, g, :].bitcast(FP8X4),
+                    lhsT_scale=xh_scales[:, g, :],
+                    rhs=w_sb[gi][:, g, cols].bitcast(FP8X4),
+                    rhs_scale=planes[k:P, gi, g // 4, cols],
+                    start=(g == 0), stop=(g == G - 1))
+
+        def add_bias(gi, hf, banks):
+            nc.vector.tensor_tensor(out=gate_sb[gi][:, hf, :, :], in0=permuted(banks[hf]),
+                                    in1=bias_bc[:, gi, hf, :, :], op=ALU.add)
+
+        def squash(gi, hf):
+            nc.scalar.activation(out=gate_sb[gi][:, hf, :, :], in_=gate_sb[gi][:, hf, :, :],
+                                 func=funcs[gi])
+
+        def to_rows(src, hf, bank):
+            for l in range(L):
+                nc.tensor.transpose(slots(bank)[:, l, :], src[:, hf, l, :], ident[:])
+
+        def rows_out(bank, z, hf, copy):
+            copy(out=z[:, hf, :, :, :],
+                 in_=bank[:].rearrange("p (l b f) -> p b l f", l=L, b=B))
+
+        def store_rows(dram, z, hf):
+            nc.sync.dma_start(
+                out=dram.rearrange("b (hf hh l) f -> hf hh b (l f)", hf=2, hh=P, l=L)[hf],
+                in_=z[:, hf, :, :, :].rearrange("p b l f -> p b (l f)"))
 
         x_words = x_sb[:].bitcast(F32)
         for g in range(GX):
             for u in range(2):
-                nc.tensor.transpose(bank[g // 2][:, (g % 2) * 2 + u, :],
+                nc.tensor.transpose(slots(tmp[g // 2])[:, (g % 2) * 2 + u, :],
                                     x_words[:, 256 * g + u:256 * (g + 1):2], ident[:])
-
         grouped_w = grouped[:].bitcast(F32)
 
         def x_src(j):
-            return bank[j][:].rearrange("p (g u) c -> p g c u", u=2)
+            return tmp[j][:].rearrange("p (g u c) -> p g c u", g=2, u=2)
 
         def quantise(half):
             gs = slice(4 * half, 4 * half + 4)
@@ -128,83 +174,86 @@ def tile_batchedlstm_w_kernel(
         nc.vector.tensor_copy(out=grouped_w[:, 0:2, :, :], in_=x_src(0))
         nc.scalar.copy(out=grouped_w[:, 2:4, :, :], in_=x_src(1))
         nc.vector.tensor_copy(out=grouped_w[:, 4:6, :, :], in_=x_src(2))
-        nc.vector.tensor_copy(out=b_f32[:], in_=b_raw[:])
-        nc.tensor.transpose(bank[3][:, 0, :], b_f32[:], ident[:])
         quantise(0)
-        nc.vector.tensor_copy(out=bias_sb[:], in_=bank[3][:, 0, 0:32])
         nc.vector.tensor_copy(
             out=grouped[:, GX:G, :, :].rearrange("p g (b f) t -> p (g b) f t", b=B),
             in_=h_raw[:].rearrange("p g b (t f) -> p (g b) f t", t=4))
+        bias_unit(0, 0, acc[2], nc.scalar.copy)
+        bias_unit(0, 1, acc[3], nc.scalar.copy)
         quantise(1)
-
-        def passes(gi, g, chunks):
-            k = 4 * (g % 4)
-            for hc in chunks:
-                cols = slice(hc * P, (hc + 1) * P)
-                nc.tensor.matmul_mx(
-                    out=bank[hc][:, gi, :],
-                    lhsT=w_sb[gi][:, g, cols].bitcast(FP8X4),
-                    lhsT_scale=planes[k:P, gi, g // 4, cols],
-                    rhs=xh_codes[:, g, :].bitcast(FP8X4),
-                    rhs_scale=xh_scales[:, g, :],
-                    start=(g == 0), stop=(g == G - 1))
-
-        def activate(gi, chunks):
-            for hc in chunks:
-                nc.scalar.activation(
-                    out=gate_sb[gi][:, hc, :], in_=bank[hc][:, gi, :], func=funcs[gi],
-                    bias=bias_sb[:, 8 * gi + hc:8 * gi + hc + 1], scale=1.0)
-
-        allc = list(range(NCH))
-        for g in range(G):
-            passes(0, g, allc)
-        activate(0, allc)
-        nc.vector.tensor_tensor(out=gate_sb[0][:], in0=gate_sb[0][:], in1=c_sb[:], op=ALU.mult)
-        for g in range(G):
-            passes(1, g, allc)
-        activate(1, allc)
-        for g in range(G):
-            passes(2, g, allc)
-        activate(2, allc)
-        for half in range(2):
-            hs = slice(4 * half, 4 * half + 4)
-            nc.vector.tensor_tensor(out=gate_sb[1][:, hs, :], in0=gate_sb[1][:, hs, :],
-                                    in1=gate_sb[2][:, hs, :], op=ALU.mult)
-            nc.vector.tensor_tensor(out=nc_sb[:, hs, :], in0=gate_sb[0][:, hs, :],
-                                    in1=gate_sb[1][:, hs, :], op=ALU.add)
-            nc.scalar.activation(out=th_sb[:, hs, :], in_=nc_sb[:, hs, :], func=ACT.Tanh)
-        for b in range(B):
-            nc.sync.dma_start(out=out_2[b].rearrange("(c p) f -> p c f", p=P),
-                              in_=nc_sb[:, :, b * F:(b + 1) * F])
+        bias_unit(1, 0, tmp[3], nc.scalar.copy)
+        bias_unit(1, 1, tmp[0], nc.scalar.copy)
+        nc.vector.tensor_copy(
+            out=c_f32[:].rearrange("p hf l (b f) -> p (hf l) b f", b=B),
+            in_=c_raw[:].rearrange("p (b hf) (l f) -> p (hf l) b f", b=B, l=L))
 
         for g in range(G):
-            passes(3, g, allc)
-        activate(3, allc)
+            passes(0, g, acc[0:2], (0, 1))
+        for hf in range(2):
+            add_bias(0, hf, acc[0:2])
+            squash(0, hf)
+        for hf in range(2):
+            for l in range(L):
+                nc.tensor.transpose(slots(tmp[1 + hf])[:, l, :], c_f32[:, hf, l, :], ident[:])
+        bias_unit(2, 0, tmp[3], nc.scalar.copy)
+        bias_unit(2, 1, tmp[0], nc.scalar.copy)
+        for hf in range(2):
+            nc.vector.tensor_tensor(out=gate_sb[0][:, hf, :, :], in0=gate_sb[0][:, hf, :, :],
+                                    in1=slots(tmp[1 + hf]), op=ALU.mult)
 
+        for g in range(G):
+            passes(1, g, acc[2:4], (0, 1))
+        for hf in range(2):
+            add_bias(1, hf, acc[2:4])
+            squash(1, hf)
+        bias_unit(3, 0, tmp[1], nc.scalar.copy)
+        bias_unit(3, 1, tmp[2], nc.scalar.copy)
+
+        for g in range(G):
+            passes(2, g, acc[0:2], (0, 1))
+        for hf in range(2):
+            add_bias(2, hf, acc[0:2])
+            squash(2, hf)
+        passes(3, 0, acc[2:4], (0, 1))
+        passes(3, 1, acc[2:4], (0, 1))
+        for hf in range(2):
+            nc.vector.tensor_tensor(out=gate_sb[1][:, hf, :, :], in0=gate_sb[1][:, hf, :, :],
+                                    in1=gate_sb[2][:, hf, :, :], op=ALU.mult)
+            nc.vector.tensor_tensor(out=gate_sb[0][:, hf, :, :], in0=gate_sb[0][:, hf, :, :],
+                                    in1=gate_sb[1][:, hf, :, :], op=ALU.add)
+            to_rows(gate_sb[0], hf, tmp[3 * hf])
+            nc.scalar.activation(out=natural_view(gate_sb[2], hf),
+                                 in_=gate_sb[0][:, hf, :, :].rearrange("p l hh -> p hh l"),
+                                 func=ACT.Tanh)
+            rows_out(tmp[3 * hf], z_cell, hf, nc.scalar.copy)
+            store_rows(out_2, z_cell, hf)
+            nc.scalar.activation(out=z_tanh[:, hf, :, :, :], in_=z_cell[:, hf, :, :, :], func=ACT.Tanh)
+            passes(3, 2 + hf, acc[2:4], (0, 1))
+
+        for g in range(4, G):
+            passes(3, g, acc[2:4], (0, 1))
         out_0_rows = out_0.rearrange("b f h -> (b f) h")
 
-        def product(j):
-            cs = slice(2 * j, 2 * j + 2)
-            nc.vector.tensor_tensor(out=nh_sb[:, cs, :], in0=th_sb[:, cs, :],
-                                    in1=gate_sb[3][:, cs, :], op=ALU.mult)
-            for b in range(B):
-                nc.sync.dma_start(
-                    out=out_1[b].rearrange("(c p) f -> p c f", p=P)[:, cs, :],
-                    in_=nh_sb[:, cs, b * F:(b + 1) * F])
-            for u in range(2):
-                nc.tensor.transpose(bank[2 * j][:, u, :], nh_sb[:, 2 * j + u, :], ident[:])
+        def hidden_natural(hf, eng):
+            eng.tensor_tensor(out=natural_view(gate_sb[1], hf),
+                              in0=gate_sb[3][:, hf, :, :].rearrange("p l hh -> p hh l"),
+                              in1=natural_view(gate_sb[2], hf), op=ALU.mult)
+            nc.sync.dma_start(out=out_0_rows[:, hf * HALF:(hf + 1) * HALF],
+                              in_=gate_sb[1][:, hf, :, :].rearrange("p l hh -> p (l hh)"))
 
-        def leave(j, eng_copy):
-            cs = slice(2 * j, 2 * j + 2)
-            eng_copy(out=o0_sb[:, cs, :], in_=bank[2 * j][:, 0:2, :])
-            nc.sync.dma_start(out=out_0_rows[:, 2 * j * P:(2 * j + 2) * P],
-                              in_=o0_sb[:, cs, :].rearrange("p c m -> p (c m)"))
+        def hidden_rows(hf):
+            nc.vector.tensor_tensor(
+                out=z_hid[:, hf, :, :, :],
+                in0=tmp[1 + hf][:].rearrange("p (l b f) -> p b l f", l=L, b=B),
+                in1=z_tanh[:, hf, :, :, :], op=ALU.mult)
+            store_rows(out_1, z_hid, hf)
 
-        product(0)
-        product(1)
-        leave(0, nc.vector.tensor_copy)
-        product(2)
-        leave(1, nc.vector.tensor_copy)
-        product(3)
-        leave(2, nc.scalar.copy)
-        leave(3, nc.scalar.copy)
+        add_bias(3, 0, acc[2:4])
+        add_bias(3, 1, acc[2:4])
+        for hf in range(2):
+            squash(3, hf)
+            to_rows(gate_sb[3], hf, tmp[1 + hf])
+        hidden_natural(0, nc.vector)
+        hidden_rows(0)
+        hidden_rows(1)
+        hidden_natural(1, nc.gpsimd)

@@ -17,10 +17,10 @@ B, F, C, H = 2, 64, 3072, 1024
 K = C + H
 G = K // 512
 GX = C // 512
-HALF = 512
-L = HALF // P
+NCH = H // P
 FLOPS = 2 * 4 * H * K * B * F
-SCALES_ON_SYNC = []
+LAST_SPLIT = 4
+SCALES_ON_SYNC = [0]
 
 
 def tile_batchedlstm_w_kernel(
@@ -50,119 +50,80 @@ def tile_batchedlstm_w_kernel(
         xh_codes = keep.tile([P, G, P], U32, name="xh_codes", align_bytes=64)
         xh_scales = keep.tile([P, G, P], U8, name="xh_scales", align_bytes=64)
         ident = keep.tile([P, P], F32, name="ident")
-        ones = keep.tile([P, P], BF16, name="ones")
-        b_row = keep.tile([P, 4, H], BF16, name="b_row")
-        bias_bc = keep.tile([P, 4, 2, L, P], F32, name="bias_bc")
-        c_raw = keep.tile([P, B * 2, L * F], BF16, name="c_raw")
-        c_f32 = keep.tile([P, 2, L, P], F32, name="c_f32")
-        gate_sb = [keep.tile([P, 2, L, P], F32, name="gate%d" % gi) for gi in range(4)]
-        z_cell = keep.tile([P, 2, B, L, F], F32, name="z_cell")
-        z_hid = keep.tile([P, 2, B, L, F], F32, name="z_hid")
-        z_tanh = keep.tile([P, 2, B, L, F], F32, name="z_tanh")
-        acc = [psum.tile([P, HALF], F32, name="acc%d" % j) for j in range(4)]
-        tmp = [psum.tile([P, HALF], F32, name="tmp%d" % j) for j in range(4)]
-
-        def slots(bank):
-            return bank[:].rearrange("p (a c) -> p a c", a=4)
-
-        def permuted(bank):
-            return bank[:].rearrange("p (hh l) -> p l hh", l=L)
-
-        def natural_view(t, hf):
-            return t[:, hf, :, :].rearrange("p l hh -> p (l hh)").rearrange("p (hh l) -> p hh l", l=L)
+        b_raw = keep.tile([P, P], BF16, name="b_raw")
+        b_f32 = keep.tile([P, P], F32, name="b_f32")
+        bias_sb = keep.tile([P, 32], F32, name="bias_sb")
+        c_sb = keep.tile([P, NCH, P], BF16, name="c_sb")
+        gate_sb = [keep.tile([P, NCH, P], F32, name="gate%d" % gi) for gi in range(4)]
+        nc_sb = keep.tile([P, NCH, P], F32, name="nc_sb")
+        th_sb = keep.tile([P, NCH, P], F32, name="th_sb")
+        nh_sb = keep.tile([P, NCH, P], F32, name="nh_sb")
+        o0_sb = keep.tile([P, NCH, P], F32, name="o0_sb")
+        bank = [psum.tile([P, 4, P], F32, name="bank%d" % j) for j in range(8)]
 
         nc.vector.memset(planes[:].rearrange("p a b n -> p (a b n)").bitcast(I32), 0)
-        nc.vector.memset(b_row[:].rearrange("p a n -> p (a n)").bitcast(I32), 0)
-        nc.vector.memset(ones[:], 1.0)
+        nc.vector.memset(b_raw[:], 0.0)
         make_identity(nc, ident[:])
 
-        def load_scales(gi):
-            for gh in range(2):
-                for q in range(4):
-                    dst = planes[32 * q:32 * q + 16, gi, gh, :]
-                    src = scales[gi][4 * gh:4 * gh + 4, 4 * q:4 * q + 4, :]
-                    if gi in SCALES_ON_SYNC:
-                        nc.sync.dma_start(out=dst.bitcast(I32), in_=src.bitcast(I32))
-                    else:
-                        nc.gpsimd.dma_start(out=dst.bitcast(F32), in_=src.bitcast(F32))
+        def load_bias(gi):
+            nc.sync.dma_start(out=b_raw[8 * gi:8 * gi + 8, :],
+                              in_=biases[gi].rearrange("(c p) -> c p", p=P))
+
+        def load_scale(gi, j):
+            gh, q = divmod(j, 4)
+            dst = planes[32 * q:32 * q + 16, gi, gh, :]
+            src = scales[gi][4 * gh:4 * gh + 4, 4 * q:4 * q + 4, :]
+            if gi in SCALES_ON_SYNC:
+                nc.sync.dma_start(out=dst.bitcast(I32), in_=src.bitcast(I32))
+            else:
+                nc.gpsimd.dma_start(out=dst.bitcast(F32), in_=src.bitcast(F32))
 
         def load_words(gi, g0, g1, n0, n1):
             nc.sync.dma_start(
                 out=w_sb[gi][:, g0:g1, n0:n1].bitcast(I32),
                 in_=words[gi][g0:g1].rearrange("g p n t -> p g (n t)")[:, :, 4 * n0:4 * n1].bitcast(I32))
 
-        nc.sync.dma_start(out=x_sb[:], in_=x.rearrange("b f c -> (b f) c"))
-        for gi in range(4):
-            nc.sync.dma_start(out=b_row[0:1, gi, :],
-                              in_=biases[gi].rearrange("(o n) -> o n", o=1))
-        for gi in range(4):
-            load_scales(gi)
-        for g in range(3):
-            load_words(0, g, g + 1, 0, H)
-        for b in range(B):
+        def load_hidden(b):
             nc.sync.dma_start(
                 out=h_raw[:, :, b, :],
                 in_=hidden_state[b].rearrange("(g p t) f -> p g (t f)", g=2, p=P, t=4))
-        nc.sync.dma_start(
-            out=c_raw[:],
-            in_=cell_state.rearrange("b (hf hh l) f -> hh (b hf) (l f)", hf=2, hh=P, l=L))
-        for g in range(3, G):
+
+        for gi in range(1, 4):
+            for j in range(8):
+                load_scale(gi, j)
+        nc.sync.dma_start(out=x_sb[:], in_=x.rearrange("b f c -> (b f) c"))
+        small = [lambda: load_scale(0, 0), lambda: load_scale(0, 1), lambda: load_scale(0, 2),
+                 lambda: load_scale(0, 3), lambda: load_hidden(0), lambda: load_hidden(1),
+                 lambda: load_scale(0, 4), lambda: load_scale(0, 5), lambda: load_scale(0, 6),
+                 lambda: load_scale(0, 7), lambda: load_bias(0), lambda: load_bias(1),
+                 lambda: load_bias(2), lambda: load_bias(3)]
+        for g in range(G):
             load_words(0, g, g + 1, 0, H)
+            for issue in small[2 * g:2 * g + 2]:
+                issue()
+        for b in range(B):
+            nc.sync.dma_start(
+                out=c_sb[:, :, b * F:(b + 1) * F],
+                in_=cell_state[b].rearrange("(c p) f -> p c f", p=P))
         for gi in (1, 2):
             for g in range(G):
                 load_words(gi, g, g + 1, 0, H)
         for g in range(G - 1):
             load_words(3, g, g + 1, 0, H)
-        for hf in range(2):
-            load_words(3, G - 1, G, hf * HALF, (hf + 1) * HALF)
-
-        def bias_unit(gi, hf, bank, copy):
-            nc.tensor.matmul(out=bank[:], lhsT=ones[:], rhs=b_row[:, gi, hf * HALF:(hf + 1) * HALF],
-                             start=True, stop=True)
-            copy(out=bias_bc[:, gi, hf, :, :], in_=permuted(bank))
-
-        def passes(gi, g, banks, halves):
-            k = 4 * (g % 4)
-            for hf in halves:
-                cols = slice(hf * HALF, (hf + 1) * HALF)
-                nc.tensor.matmul_mx(
-                    out=banks[hf][:],
-                    lhsT=xh_codes[:, g, :].bitcast(FP8X4),
-                    lhsT_scale=xh_scales[:, g, :],
-                    rhs=w_sb[gi][:, g, cols].bitcast(FP8X4),
-                    rhs_scale=planes[k:P, gi, g // 4, cols],
-                    start=(g == 0), stop=(g == G - 1))
-
-        def add_bias(gi, hf, banks):
-            nc.vector.tensor_tensor(out=gate_sb[gi][:, hf, :, :], in0=permuted(banks[hf]),
-                                    in1=bias_bc[:, gi, hf, :, :], op=ALU.add)
-
-        def squash(gi, hf):
-            nc.scalar.activation(out=gate_sb[gi][:, hf, :, :], in_=gate_sb[gi][:, hf, :, :],
-                                 func=funcs[gi])
-
-        def to_rows(src, hf, bank):
-            for l in range(L):
-                nc.tensor.transpose(slots(bank)[:, l, :], src[:, hf, l, :], ident[:])
-
-        def rows_out(bank, z, hf, copy):
-            copy(out=z[:, hf, :, :, :],
-                 in_=bank[:].rearrange("p (l b f) -> p b l f", l=L, b=B))
-
-        def store_rows(dram, z, hf):
-            nc.sync.dma_start(
-                out=dram.rearrange("b (hf hh l) f -> hf hh b (l f)", hf=2, hh=P, l=L)[hf],
-                in_=z[:, hf, :, :, :].rearrange("p b l f -> p b (l f)"))
+        for s in range(LAST_SPLIT):
+            w = H // LAST_SPLIT
+            load_words(3, G - 1, G, s * w, (s + 1) * w)
 
         x_words = x_sb[:].bitcast(F32)
         for g in range(GX):
             for u in range(2):
-                nc.tensor.transpose(slots(tmp[g // 2])[:, (g % 2) * 2 + u, :],
+                nc.tensor.transpose(bank[g // 2][:, (g % 2) * 2 + u, :],
                                     x_words[:, 256 * g + u:256 * (g + 1):2], ident[:])
+
         grouped_w = grouped[:].bitcast(F32)
 
         def x_src(j):
-            return tmp[j][:].rearrange("p (g u c) -> p g c u", g=2, u=2)
+            return bank[j][:].rearrange("p (g u) c -> p g c u", u=2)
 
         def quantise(half):
             gs = slice(4 * half, 4 * half + 4)
@@ -178,82 +139,79 @@ def tile_batchedlstm_w_kernel(
         nc.vector.tensor_copy(
             out=grouped[:, GX:G, :, :].rearrange("p g (b f) t -> p (g b) f t", b=B),
             in_=h_raw[:].rearrange("p g b (t f) -> p (g b) f t", t=4))
-        bias_unit(0, 0, acc[2], nc.scalar.copy)
-        bias_unit(0, 1, acc[3], nc.scalar.copy)
         quantise(1)
-        bias_unit(1, 0, tmp[3], nc.scalar.copy)
-        bias_unit(1, 1, tmp[0], nc.scalar.copy)
-        nc.vector.tensor_copy(
-            out=c_f32[:].rearrange("p hf l (b f) -> p (hf l) b f", b=B),
-            in_=c_raw[:].rearrange("p (b hf) (l f) -> p (hf l) b f", b=B, l=L))
+        nc.vector.tensor_copy(out=b_f32[:], in_=b_raw[:])
+
+        def passes(gi, g, chunks):
+            k = 4 * (g % 4)
+            for hc in chunks:
+                cols = slice(hc * P, (hc + 1) * P)
+                nc.tensor.matmul_mx(
+                    out=bank[hc][:, gi, :],
+                    lhsT=w_sb[gi][:, g, cols].bitcast(FP8X4),
+                    lhsT_scale=planes[k:P, gi, g // 4, cols],
+                    rhs=xh_codes[:, g, :].bitcast(FP8X4),
+                    rhs_scale=xh_scales[:, g, :],
+                    start=(g == 0), stop=(g == G - 1))
+
+        def activate(gi, chunks):
+            for hc in chunks:
+                nc.scalar.activation(
+                    out=gate_sb[gi][:, hc, :], in_=bank[hc][:, gi, :], func=funcs[gi],
+                    bias=bias_sb[:, 8 * gi + hc:8 * gi + hc + 1], scale=1.0)
+
+        allc = list(range(NCH))
+        for g in range(G):
+            passes(0, g, allc)
+        nc.tensor.transpose(bank[3][:, 3, :], b_f32[:], ident[:])
+        nc.vector.tensor_copy(out=bias_sb[:], in_=bank[3][:, 3, 0:32])
+        activate(0, allc)
+        nc.vector.tensor_tensor(out=gate_sb[0][:], in0=gate_sb[0][:], in1=c_sb[:], op=ALU.mult)
+        for g in range(G):
+            passes(1, g, allc)
+        activate(1, allc)
+        for g in range(G):
+            passes(2, g, allc)
+        activate(2, allc)
+        for half in range(2):
+            hs = slice(4 * half, 4 * half + 4)
+            nc.vector.tensor_tensor(out=gate_sb[1][:, hs, :], in0=gate_sb[1][:, hs, :],
+                                    in1=gate_sb[2][:, hs, :], op=ALU.mult)
+            nc.vector.tensor_tensor(out=nc_sb[:, hs, :], in0=gate_sb[0][:, hs, :],
+                                    in1=gate_sb[1][:, hs, :], op=ALU.add)
+            nc.scalar.activation(out=th_sb[:, hs, :], in_=nc_sb[:, hs, :], func=ACT.Tanh)
+        for b in range(B):
+            nc.sync.dma_start(out=out_2[b].rearrange("(c p) f -> p c f", p=P),
+                              in_=nc_sb[:, :, b * F:(b + 1) * F])
 
         for g in range(G):
-            passes(0, g, acc[0:2], (0, 1))
-        for hf in range(2):
-            add_bias(0, hf, acc[0:2])
-            squash(0, hf)
-        for hf in range(2):
-            for l in range(L):
-                nc.tensor.transpose(slots(tmp[1 + hf])[:, l, :], c_f32[:, hf, l, :], ident[:])
-        bias_unit(2, 0, tmp[3], nc.scalar.copy)
-        bias_unit(2, 1, tmp[0], nc.scalar.copy)
-        for hf in range(2):
-            nc.vector.tensor_tensor(out=gate_sb[0][:, hf, :, :], in0=gate_sb[0][:, hf, :, :],
-                                    in1=slots(tmp[1 + hf]), op=ALU.mult)
+            passes(3, g, allc)
+        activate(3, allc)
 
-        for g in range(G):
-            passes(1, g, acc[2:4], (0, 1))
-        for hf in range(2):
-            add_bias(1, hf, acc[2:4])
-            squash(1, hf)
-        bias_unit(3, 0, tmp[1], nc.scalar.copy)
-        bias_unit(3, 1, tmp[2], nc.scalar.copy)
-
-        for g in range(G):
-            passes(2, g, acc[0:2], (0, 1))
-        for hf in range(2):
-            add_bias(2, hf, acc[0:2])
-            squash(2, hf)
-        passes(3, 0, acc[2:4], (0, 1))
-        passes(3, 1, acc[2:4], (0, 1))
-        for hf in range(2):
-            nc.vector.tensor_tensor(out=gate_sb[1][:, hf, :, :], in0=gate_sb[1][:, hf, :, :],
-                                    in1=gate_sb[2][:, hf, :, :], op=ALU.mult)
-            nc.vector.tensor_tensor(out=gate_sb[0][:, hf, :, :], in0=gate_sb[0][:, hf, :, :],
-                                    in1=gate_sb[1][:, hf, :, :], op=ALU.add)
-            to_rows(gate_sb[0], hf, tmp[3 * hf])
-            nc.scalar.activation(out=natural_view(gate_sb[2], hf),
-                                 in_=gate_sb[0][:, hf, :, :].rearrange("p l hh -> p hh l"),
-                                 func=ACT.Tanh)
-            rows_out(tmp[3 * hf], z_cell, hf, nc.scalar.copy)
-            store_rows(out_2, z_cell, hf)
-            nc.scalar.activation(out=z_tanh[:, hf, :, :, :], in_=z_cell[:, hf, :, :, :], func=ACT.Tanh)
-            passes(3, 2 + hf, acc[2:4], (0, 1))
-
-        for g in range(4, G):
-            passes(3, g, acc[2:4], (0, 1))
         out_0_rows = out_0.rearrange("b f h -> (b f) h")
 
-        def hidden_natural(hf, eng):
-            eng.tensor_tensor(out=natural_view(gate_sb[1], hf),
-                              in0=gate_sb[3][:, hf, :, :].rearrange("p l hh -> p hh l"),
-                              in1=natural_view(gate_sb[2], hf), op=ALU.mult)
-            nc.sync.dma_start(out=out_0_rows[:, hf * HALF:(hf + 1) * HALF],
-                              in_=gate_sb[1][:, hf, :, :].rearrange("p l hh -> p (l hh)"))
+        def product(j):
+            cs = slice(2 * j, 2 * j + 2)
+            nc.vector.tensor_tensor(out=nh_sb[:, cs, :], in0=th_sb[:, cs, :],
+                                    in1=gate_sb[3][:, cs, :], op=ALU.mult)
+            for b in range(B):
+                nc.sync.dma_start(
+                    out=out_1[b].rearrange("(c p) f -> p c f", p=P)[:, cs, :],
+                    in_=nh_sb[:, cs, b * F:(b + 1) * F])
+            for u in range(2):
+                nc.tensor.transpose(bank[2 * j][:, u, :], nh_sb[:, 2 * j + u, :], ident[:])
 
-        def hidden_rows(hf):
-            nc.vector.tensor_tensor(
-                out=z_hid[:, hf, :, :, :],
-                in0=tmp[1 + hf][:].rearrange("p (l b f) -> p b l f", l=L, b=B),
-                in1=z_tanh[:, hf, :, :, :], op=ALU.mult)
-            store_rows(out_1, z_hid, hf)
+        def leave(j, eng_copy):
+            cs = slice(2 * j, 2 * j + 2)
+            eng_copy(out=o0_sb[:, cs, :], in_=bank[2 * j][:, 0:2, :])
+            nc.sync.dma_start(out=out_0_rows[:, 2 * j * P:(2 * j + 2) * P],
+                              in_=o0_sb[:, cs, :].rearrange("p c m -> p (c m)"))
 
-        add_bias(3, 0, acc[2:4])
-        add_bias(3, 1, acc[2:4])
-        for hf in range(2):
-            squash(3, hf)
-            to_rows(gate_sb[3], hf, tmp[1 + hf])
-        hidden_natural(0, nc.vector)
-        hidden_rows(0)
-        hidden_rows(1)
-        hidden_natural(1, nc.gpsimd)
+        product(0)
+        product(1)
+        leave(0, nc.vector.tensor_copy)
+        product(2)
+        leave(1, nc.vector.tensor_copy)
+        product(3)
+        leave(2, nc.scalar.copy)
+        leave(3, nc.scalar.copy)

@@ -20,7 +20,7 @@ GX = C // 512
 NCH = H // P
 FLOPS = 2 * 4 * H * K * B * F
 LAST_SPLIT = 4
-SCALES_ON_SYNC = [0]
+SCALES_ON_SYNC = [0, 1, 2, 3]
 
 
 def tile_batchedlstm_w_kernel(
@@ -88,26 +88,27 @@ def tile_batchedlstm_w_kernel(
                 out=h_raw[:, :, b, :],
                 in_=hidden_state[b].rearrange("(g p t) f -> p g (t f)", g=2, p=P, t=4))
 
-        for gi in range(1, 4):
-            for j in range(8):
-                load_scale(gi, j)
-        nc.sync.dma_start(out=x_sb[:], in_=x.rearrange("b f c -> (b f) c"))
-        small = [lambda: load_scale(0, 0), lambda: load_scale(0, 1), lambda: load_scale(0, 2),
-                 lambda: load_scale(0, 3), lambda: load_hidden(0), lambda: load_hidden(1),
-                 lambda: load_scale(0, 4), lambda: load_scale(0, 5), lambda: load_scale(0, 6),
-                 lambda: load_scale(0, 7), lambda: load_bias(0), lambda: load_bias(1),
-                 lambda: load_bias(2), lambda: load_bias(3)]
-        for g in range(G):
-            load_words(0, g, g + 1, 0, H)
-            for issue in small[2 * g:2 * g + 2]:
-                issue()
-        for b in range(B):
+        def load_cell(b):
             nc.sync.dma_start(
                 out=c_sb[:, :, b * F:(b + 1) * F],
                 in_=cell_state[b].rearrange("(c p) f -> p c f", p=P))
-        for gi in (1, 2):
+
+        def sc(gi, j):
+            return lambda: load_scale(gi, j)
+
+        small = ([sc(0, j) for j in range(4)] + [lambda: load_hidden(0), lambda: load_hidden(1)]
+                 + [sc(0, j) for j in range(4, 8)]
+                 + [lambda: load_bias(0), lambda: load_bias(1), lambda: load_bias(2), lambda: load_bias(3)]
+                 + [lambda: load_cell(0), lambda: load_cell(1)]
+                 + [sc(gi, j) for gi in (1, 2, 3) for j in range(8)])
+        nc.sync.dma_start(out=x_sb[:], in_=x.rearrange("b f c -> (b f) c"))
+        slab = 0
+        for gi in range(3):
             for g in range(G):
                 load_words(gi, g, g + 1, 0, H)
+                for issue in small[2 * slab:2 * slab + 2]:
+                    issue()
+                slab += 1
         for g in range(G - 1):
             load_words(3, g, g + 1, 0, H)
         for s in range(LAST_SPLIT):

@@ -20,7 +20,7 @@ GX = C // 512
 NCH = H // P
 FLOPS = 2 * 4 * H * K * B * F
 LAST_SPLIT = 4
-SCALES_ON_SYNC = [0, 1, 2, 3]
+SCALES_ON_SYNC = [0]
 
 
 def tile_batchedlstm_w_kernel(
@@ -53,7 +53,12 @@ def tile_batchedlstm_w_kernel(
         b_raw = keep.tile([P, P], BF16, name="b_raw")
         b_f32 = keep.tile([P, P], F32, name="b_f32")
         bias_sb = keep.tile([P, 32], F32, name="bias_sb")
-        c_sb = keep.tile([P, NCH, P], BF16, name="c_sb")
+        c_raw = keep.tile([P, B, 8 * F], BF16, name="c_raw")
+        c_f32 = keep.tile([P, 8, P], F32, name="c_f32")
+        c_tok = keep.tile([P, H], F32, name="c_tok")
+        c_sb = keep.tile([P, NCH, P], F32, name="c_sb")
+        nc_tok = keep.tile([P, 8, P], F32, name="nc_tok")
+        z_cell = keep.tile([P, B, 8, F], F32, name="z_cell")
         gate_sb = [keep.tile([P, NCH, P], F32, name="gate%d" % gi) for gi in range(4)]
         nc_sb = keep.tile([P, NCH, P], F32, name="nc_sb")
         th_sb = keep.tile([P, NCH, P], F32, name="th_sb")
@@ -88,27 +93,23 @@ def tile_batchedlstm_w_kernel(
                 out=h_raw[:, :, b, :],
                 in_=hidden_state[b].rearrange("(g p t) f -> p g (t f)", g=2, p=P, t=4))
 
-        def load_cell(b):
-            nc.sync.dma_start(
-                out=c_sb[:, :, b * F:(b + 1) * F],
-                in_=cell_state[b].rearrange("(c p) f -> p c f", p=P))
-
-        def sc(gi, j):
-            return lambda: load_scale(gi, j)
-
-        small = ([sc(0, j) for j in range(4)] + [lambda: load_hidden(0), lambda: load_hidden(1)]
-                 + [sc(0, j) for j in range(4, 8)]
-                 + [lambda: load_bias(0), lambda: load_bias(1), lambda: load_bias(2), lambda: load_bias(3)]
-                 + [lambda: load_cell(0), lambda: load_cell(1)]
-                 + [sc(gi, j) for gi in (1, 2, 3) for j in range(8)])
+        for gi in range(1, 4):
+            for j in range(8):
+                load_scale(gi, j)
         nc.sync.dma_start(out=x_sb[:], in_=x.rearrange("b f c -> (b f) c"))
-        slab = 0
-        for gi in range(3):
+        nc.sync.dma_start(out=c_raw[:], in_=cell_state.rearrange("b (hh l) f -> hh b (l f)", l=8))
+        small = [lambda: load_scale(0, 0), lambda: load_scale(0, 1), lambda: load_scale(0, 2),
+                 lambda: load_scale(0, 3), lambda: load_hidden(0), lambda: load_hidden(1),
+                 lambda: load_scale(0, 4), lambda: load_scale(0, 5), lambda: load_scale(0, 6),
+                 lambda: load_scale(0, 7), lambda: load_bias(0), lambda: load_bias(1),
+                 lambda: load_bias(2), lambda: load_bias(3)]
+        for g in range(G):
+            load_words(0, g, g + 1, 0, H)
+            for issue in small[2 * g:2 * g + 2]:
+                issue()
+        for gi in (1, 2):
             for g in range(G):
                 load_words(gi, g, g + 1, 0, H)
-                for issue in small[2 * slab:2 * slab + 2]:
-                    issue()
-                slab += 1
         for g in range(G - 1):
             load_words(3, g, g + 1, 0, H)
         for s in range(LAST_SPLIT):
@@ -133,6 +134,8 @@ def tile_batchedlstm_w_kernel(
                 scales=xh_scales[:, gs, :].rearrange("p g c -> p (g c)"),
                 in_=grouped[:, gs, :, :].rearrange("p g c t -> p (g c t)"))
 
+        nc.scalar.copy(out=c_f32[:].rearrange("p l (b f) -> p l b f", b=B),
+                       in_=c_raw[:].rearrange("p b (l f) -> p l b f", l=8))
         nc.vector.tensor_copy(out=grouped_w[:, 0:2, :, :], in_=x_src(0))
         nc.scalar.copy(out=grouped_w[:, 2:4, :, :], in_=x_src(1))
         nc.vector.tensor_copy(out=grouped_w[:, 4:6, :, :], in_=x_src(2))
@@ -141,6 +144,15 @@ def tile_batchedlstm_w_kernel(
             out=grouped[:, GX:G, :, :].rearrange("p g (b f) t -> p (g b) f t", b=B),
             in_=h_raw[:].rearrange("p g b (t f) -> p (g b) f t", t=4))
         quantise(1)
+        for l in range(8):
+            nc.tensor.transpose(bank[4 + l // 4][:, l % 4, :], c_f32[:, l, :], ident[:])
+        for j in range(2):
+            nc.scalar.copy(out=c_tok[:].rearrange("p (hh l) -> p hh l", l=8)[:, :, 4 * j:4 * j + 4],
+                           in_=bank[4 + j][:].rearrange("p l hh -> p hh l"))
+        for hc in range(NCH):
+            nc.tensor.transpose(bank[6 + hc // 4][:, hc % 4, :], c_tok[:, hc * P:(hc + 1) * P], ident[:])
+        nc.scalar.copy(out=c_sb[:, 0:4, :], in_=bank[6][:])
+        nc.vector.tensor_copy(out=c_sb[:, 4:8, :], in_=bank[7][:])
         nc.vector.tensor_copy(out=b_f32[:], in_=b_raw[:])
 
         def passes(gi, g, chunks):
@@ -174,19 +186,41 @@ def tile_batchedlstm_w_kernel(
         for g in range(G):
             passes(2, g, allc)
         activate(2, allc)
-        for half in range(2):
+        early, late = allc[0:6], allc[6:8]
+
+        def new_cell(half):
             hs = slice(4 * half, 4 * half + 4)
             nc.vector.tensor_tensor(out=gate_sb[1][:, hs, :], in0=gate_sb[1][:, hs, :],
                                     in1=gate_sb[2][:, hs, :], op=ALU.mult)
             nc.vector.tensor_tensor(out=nc_sb[:, hs, :], in0=gate_sb[0][:, hs, :],
                                     in1=gate_sb[1][:, hs, :], op=ALU.add)
             nc.scalar.activation(out=th_sb[:, hs, :], in_=nc_sb[:, hs, :], func=ACT.Tanh)
-        for b in range(B):
-            nc.sync.dma_start(out=out_2[b].rearrange("(c p) f -> p c f", p=P),
-                              in_=nc_sb[:, :, b * F:(b + 1) * F])
+            for c in range(4):
+                nc.tensor.transpose(bank[6 + half][:, c, :], nc_sb[:, 4 * half + c, :], ident[:])
 
+        def regroup(half, copy):
+            copy(out=nc_tok[:, :, 64 * half:64 * half + 64],
+                 in_=bank[6 + half][:].rearrange("p c m -> p (c m)").rearrange("p (hh l) -> p l hh", l=8))
+
+        for g in range(3):
+            passes(3, g, early)
+        new_cell(0)
+        passes(3, 3, early)
+        regroup(0, nc.scalar.copy)
+        new_cell(1)
+        regroup(1, nc.vector.tensor_copy)
+        passes(3, 4, early)
+        passes(3, 5, early)
+        for l in range(8):
+            nc.tensor.transpose(bank[6 + l // 4][:, l % 4, :], nc_tok[:, l, :], ident[:])
+        nc.scalar.copy(out=z_cell[:, :, 0:4, :], in_=bank[6][:].rearrange("p l (b f) -> p b l f", b=B))
+        nc.vector.tensor_copy(out=z_cell[:, :, 4:8, :], in_=bank[7][:].rearrange("p l (b f) -> p b l f", b=B))
+        nc.sync.dma_start(out=out_2.rearrange("b (hh l) f -> hh b (l f)", l=8),
+                          in_=z_cell[:].rearrange("p b l f -> p b (l f)"))
+        passes(3, 6, early)
+        passes(3, 7, early)
         for g in range(G):
-            passes(3, g, allc)
+            passes(3, g, late)
         activate(3, allc)
 
         out_0_rows = out_0.rearrange("b f h -> (b f) h")

@@ -53,12 +53,7 @@ def tile_batchedlstm_w_kernel(
         b_raw = keep.tile([P, P], BF16, name="b_raw")
         b_f32 = keep.tile([P, P], F32, name="b_f32")
         bias_sb = keep.tile([P, 32], F32, name="bias_sb")
-        c_raw = keep.tile([P, B, 8 * F], BF16, name="c_raw")
-        c_f32 = keep.tile([P, 8, P], F32, name="c_f32")
-        c_tok = keep.tile([P, H], F32, name="c_tok")
-        c_sb = keep.tile([P, NCH, P], F32, name="c_sb")
-        nc_tok = keep.tile([P, 8, P], F32, name="nc_tok")
-        z_cell = keep.tile([P, B, 8, F], F32, name="z_cell")
+        c_sb = keep.tile([P, NCH, P], BF16, name="c_sb")
         gate_sb = [keep.tile([P, NCH, P], F32, name="gate%d" % gi) for gi in range(4)]
         nc_sb = keep.tile([P, NCH, P], F32, name="nc_sb")
         th_sb = keep.tile([P, NCH, P], F32, name="th_sb")
@@ -97,7 +92,6 @@ def tile_batchedlstm_w_kernel(
             for j in range(8):
                 load_scale(gi, j)
         nc.sync.dma_start(out=x_sb[:], in_=x.rearrange("b f c -> (b f) c"))
-        nc.sync.dma_start(out=c_raw[:], in_=cell_state.rearrange("b (hh l) f -> hh b (l f)", l=8))
         small = [lambda: load_scale(0, 0), lambda: load_scale(0, 1), lambda: load_scale(0, 2),
                  lambda: load_scale(0, 3), lambda: load_hidden(0), lambda: load_hidden(1),
                  lambda: load_scale(0, 4), lambda: load_scale(0, 5), lambda: load_scale(0, 6),
@@ -107,6 +101,10 @@ def tile_batchedlstm_w_kernel(
             load_words(0, g, g + 1, 0, H)
             for issue in small[2 * g:2 * g + 2]:
                 issue()
+        for b in range(B):
+            nc.sync.dma_start(
+                out=c_sb[:, :, b * F:(b + 1) * F],
+                in_=cell_state[b].rearrange("(c p) f -> p c f", p=P))
         for gi in (1, 2):
             for g in range(G):
                 load_words(gi, g, g + 1, 0, H)
@@ -134,8 +132,6 @@ def tile_batchedlstm_w_kernel(
                 scales=xh_scales[:, gs, :].rearrange("p g c -> p (g c)"),
                 in_=grouped[:, gs, :, :].rearrange("p g c t -> p (g c t)"))
 
-        nc.scalar.copy(out=c_f32[:].rearrange("p l (b f) -> p l b f", b=B),
-                       in_=c_raw[:].rearrange("p b (l f) -> p l b f", l=8))
         nc.vector.tensor_copy(out=grouped_w[:, 0:2, :, :], in_=x_src(0))
         nc.scalar.copy(out=grouped_w[:, 2:4, :, :], in_=x_src(1))
         nc.vector.tensor_copy(out=grouped_w[:, 4:6, :, :], in_=x_src(2))
@@ -144,15 +140,6 @@ def tile_batchedlstm_w_kernel(
             out=grouped[:, GX:G, :, :].rearrange("p g (b f) t -> p (g b) f t", b=B),
             in_=h_raw[:].rearrange("p g b (t f) -> p (g b) f t", t=4))
         quantise(1)
-        for l in range(8):
-            nc.tensor.transpose(bank[4 + l // 4][:, l % 4, :], c_f32[:, l, :], ident[:])
-        for j in range(2):
-            nc.scalar.copy(out=c_tok[:].rearrange("p (hh l) -> p hh l", l=8)[:, :, 4 * j:4 * j + 4],
-                           in_=bank[4 + j][:].rearrange("p l hh -> p hh l"))
-        for hc in range(NCH):
-            nc.tensor.transpose(bank[6 + hc // 4][:, hc % 4, :], c_tok[:, hc * P:(hc + 1) * P], ident[:])
-        nc.scalar.copy(out=c_sb[:, 0:4, :], in_=bank[6][:])
-        nc.vector.tensor_copy(out=c_sb[:, 4:8, :], in_=bank[7][:])
         nc.vector.tensor_copy(out=b_f32[:], in_=b_raw[:])
 
         def passes(gi, g, chunks):
@@ -186,41 +173,19 @@ def tile_batchedlstm_w_kernel(
         for g in range(G):
             passes(2, g, allc)
         activate(2, allc)
-        early, late = allc[0:6], allc[6:8]
-
-        def new_cell(half):
+        for half in range(2):
             hs = slice(4 * half, 4 * half + 4)
             nc.vector.tensor_tensor(out=gate_sb[1][:, hs, :], in0=gate_sb[1][:, hs, :],
                                     in1=gate_sb[2][:, hs, :], op=ALU.mult)
             nc.vector.tensor_tensor(out=nc_sb[:, hs, :], in0=gate_sb[0][:, hs, :],
                                     in1=gate_sb[1][:, hs, :], op=ALU.add)
             nc.scalar.activation(out=th_sb[:, hs, :], in_=nc_sb[:, hs, :], func=ACT.Tanh)
-            for c in range(4):
-                nc.tensor.transpose(bank[6 + half][:, c, :], nc_sb[:, 4 * half + c, :], ident[:])
+        for b in range(B):
+            nc.sync.dma_start(out=out_2[b].rearrange("(c p) f -> p c f", p=P),
+                              in_=nc_sb[:, :, b * F:(b + 1) * F])
 
-        def regroup(half, copy):
-            copy(out=nc_tok[:, :, 64 * half:64 * half + 64],
-                 in_=bank[6 + half][:].rearrange("p c m -> p (c m)").rearrange("p (hh l) -> p l hh", l=8))
-
-        for g in range(3):
-            passes(3, g, early)
-        new_cell(0)
-        passes(3, 3, early)
-        regroup(0, nc.scalar.copy)
-        new_cell(1)
-        regroup(1, nc.vector.tensor_copy)
-        passes(3, 4, early)
-        passes(3, 5, early)
-        for l in range(8):
-            nc.tensor.transpose(bank[6 + l // 4][:, l % 4, :], nc_tok[:, l, :], ident[:])
-        nc.scalar.copy(out=z_cell[:, :, 0:4, :], in_=bank[6][:].rearrange("p l (b f) -> p b l f", b=B))
-        nc.vector.tensor_copy(out=z_cell[:, :, 4:8, :], in_=bank[7][:].rearrange("p l (b f) -> p b l f", b=B))
-        nc.sync.dma_start(out=out_2.rearrange("b (hh l) f -> hh b (l f)", l=8),
-                          in_=z_cell[:].rearrange("p b l f -> p b (l f)"))
-        passes(3, 6, early)
-        passes(3, 7, early)
         for g in range(G):
-            passes(3, g, late)
+            passes(3, g, allc)
         activate(3, allc)
 
         out_0_rows = out_0.rearrange("b f h -> (b f) h")
@@ -229,24 +194,34 @@ def tile_batchedlstm_w_kernel(
             cs = slice(2 * j, 2 * j + 2)
             nc.vector.tensor_tensor(out=nh_sb[:, cs, :], in0=th_sb[:, cs, :],
                                     in1=gate_sb[3][:, cs, :], op=ALU.mult)
+            for u in range(2):
+                nc.tensor.transpose(bank[2 * j][:, u, :], nh_sb[:, 2 * j + u, :], ident[:])
+
+        def store_hidden(q):
+            cs = slice(4 * q, 4 * q + 4)
             for b in range(B):
                 nc.sync.dma_start(
                     out=out_1[b].rearrange("(c p) f -> p c f", p=P)[:, cs, :],
                     in_=nh_sb[:, cs, b * F:(b + 1) * F])
-            for u in range(2):
-                nc.tensor.transpose(bank[2 * j][:, u, :], nh_sb[:, 2 * j + u, :], ident[:])
 
         def leave(j, eng_copy):
             cs = slice(2 * j, 2 * j + 2)
             eng_copy(out=o0_sb[:, cs, :], in_=bank[2 * j][:, 0:2, :])
-            nc.sync.dma_start(out=out_0_rows[:, 2 * j * P:(2 * j + 2) * P],
+
+        def store_tokens(q):
+            cs = slice(4 * q, 4 * q + 4)
+            nc.sync.dma_start(out=out_0_rows[:, 4 * q * P:(4 * q + 4) * P],
                               in_=o0_sb[:, cs, :].rearrange("p c m -> p (c m)"))
 
         product(0)
         product(1)
+        store_hidden(0)
         leave(0, nc.vector.tensor_copy)
         product(2)
         leave(1, nc.vector.tensor_copy)
+        store_tokens(0)
         product(3)
+        store_hidden(1)
         leave(2, nc.scalar.copy)
         leave(3, nc.scalar.copy)
+        store_tokens(1)

@@ -97,19 +97,20 @@ def tile_batchedlstm_w_kernel(
                  lambda: load_scale(0, 4), lambda: load_scale(0, 5), lambda: load_scale(0, 6),
                  lambda: load_scale(0, 7), lambda: load_bias(0), lambda: load_bias(1),
                  lambda: load_bias(2), lambda: load_bias(3)]
-        for g in range(G):
-            load_words(0, g, g + 1, 0, H)
-            for issue in small[2 * g:2 * g + 2]:
+        for g in range(0, G, 2):
+            load_words(0, g, g + 2, 0, H)
+            for issue in small[2 * g:2 * g + 4]:
                 issue()
         for b in range(B):
             nc.sync.dma_start(
                 out=c_sb[:, :, b * F:(b + 1) * F],
                 in_=cell_state[b].rearrange("(c p) f -> p c f", p=P))
         for gi in (1, 2):
-            for g in range(G):
-                load_words(gi, g, g + 1, 0, H)
-        for g in range(G - 1):
-            load_words(3, g, g + 1, 0, H)
+            for g in range(0, G, 4):
+                load_words(gi, g, g + 4, 0, H)
+        load_words(3, 0, 4, 0, H)
+        load_words(3, 4, 6, 0, H)
+        load_words(3, 6, 7, 0, H)
         for s in range(LAST_SPLIT):
             w = H // LAST_SPLIT
             load_words(3, G - 1, G, s * w, (s + 1) * w)

@@ -53,6 +53,10 @@ def tile_batchedlstm_w_kernel(
         b_raw = keep.tile([P, P], BF16, name="b_raw")
         b_f32 = keep.tile([P, P], F32, name="b_f32")
         bias_sb = keep.tile([P, 32], F32, name="bias_sb")
+        ident_bf = keep.tile([P, P], BF16, name="ident_bf")
+        c_raw = keep.tile([P, B, NCH, F], BF16, name="c_raw")
+        c_byj = keep.tile([P, NCH, P], BF16, name="c_byj")
+        c_tok = keep.tile([P, H], BF16, name="c_tok")
         c_sb = keep.tile([P, NCH, P], BF16, name="c_sb")
         gate_sb = [keep.tile([P, NCH, P], F32, name="gate%d" % gi) for gi in range(4)]
         nc_sb = keep.tile([P, NCH, P], F32, name="nc_sb")
@@ -64,6 +68,7 @@ def tile_batchedlstm_w_kernel(
         nc.vector.memset(planes[:].rearrange("p a b n -> p (a b n)").bitcast(I32), 0)
         nc.vector.memset(b_raw[:], 0.0)
         make_identity(nc, ident[:])
+        make_identity(nc, ident_bf[:])
 
         def load_bias(gi):
             nc.sync.dma_start(out=b_raw[8 * gi:8 * gi + 8, :],
@@ -92,6 +97,8 @@ def tile_batchedlstm_w_kernel(
             for j in range(8):
                 load_scale(gi, j)
         nc.sync.dma_start(out=x_sb[:], in_=x.rearrange("b f c -> (b f) c"))
+        nc.sync.dma_start(out=c_raw[:].rearrange("p b j f -> p b (j f)"),
+                          in_=cell_state.rearrange("b (p j) f -> p b (j f)", j=NCH))
         small = [lambda: load_scale(0, 0), lambda: load_scale(0, 1), lambda: load_scale(0, 2),
                  lambda: load_scale(0, 3), lambda: load_hidden(0), lambda: load_hidden(1),
                  lambda: load_scale(0, 4), lambda: load_scale(0, 5), lambda: load_scale(0, 6),
@@ -101,10 +108,6 @@ def tile_batchedlstm_w_kernel(
             load_words(0, g, g + 2, 0, H)
             for issue in small[2 * g:2 * g + 4]:
                 issue()
-        for b in range(B):
-            nc.sync.dma_start(
-                out=c_sb[:, :, b * F:(b + 1) * F],
-                in_=cell_state[b].rearrange("(c p) f -> p c f", p=P))
         for gi in (1, 2):
             for g in range(0, G, 4):
                 load_words(gi, g, g + 4, 0, H)
@@ -121,6 +124,13 @@ def tile_batchedlstm_w_kernel(
                 nc.tensor.transpose(bank[g // 2][:, (g % 2) * 2 + u, :],
                                     x_words[:, 256 * g + u:256 * (g + 1):2], ident[:])
 
+        tok_bank = bank[4][:].rearrange("p a m -> p (a m)").bitcast(BF16)
+        back_bank = bank[5][:].rearrange("p a m -> p (a m)").bitcast(BF16)
+        nc.scalar.copy(out=c_byj[:].rearrange("p j (b f) -> p j b f", b=B),
+                       in_=c_raw[:].rearrange("p b j f -> p j b f"))
+        for j in range(NCH):
+            nc.tensor.transpose(tok_bank[:, j * P:(j + 1) * P], c_byj[:, j, :], ident_bf[:])
+
         grouped_w = grouped[:].bitcast(F32)
 
         def x_src(j):
@@ -135,6 +145,11 @@ def tile_batchedlstm_w_kernel(
 
         nc.vector.tensor_copy(out=grouped_w[:, 0:2, :, :], in_=x_src(0))
         nc.scalar.copy(out=grouped_w[:, 2:4, :, :], in_=x_src(1))
+        nc.scalar.copy(out=c_tok[:].rearrange("t (p j) -> t p j", j=NCH),
+                       in_=tok_bank.rearrange("t (j p) -> t p j", j=NCH))
+        for hc in range(NCH):
+            nc.tensor.transpose(back_bank[:, hc * P:(hc + 1) * P], c_tok[:, hc * P:(hc + 1) * P], ident_bf[:])
+        nc.scalar.copy(out=c_sb[:].rearrange("p c m -> p (c m)"), in_=back_bank)
         nc.vector.tensor_copy(out=grouped_w[:, 4:6, :, :], in_=x_src(2))
         quantise(0)
         nc.vector.tensor_copy(

@@ -108,12 +108,14 @@ def tile_batchedlstm_w_kernel(
             load_words(0, g, g + 2, 0, H)
             for issue in small[2 * g:2 * g + 4]:
                 issue()
-        for gi in (1, 2):
-            for g in range(0, G, 4):
-                load_words(gi, g, g + 4, 0, H)
-        load_words(3, 0, 4, 0, H)
-        load_words(3, 4, 6, 0, H)
-        load_words(3, 6, 7, 0, H)
+        for g in range(0, G, 4):
+            load_words(1, g, g + 4, 0, H)
+        for g in range(0, G, 2):
+            load_words(2, g, g + 2, 0, H)
+        load_words(3, 0, 2, 0, H)
+        load_words(3, 2, 4, 0, H)
+        for g in range(4, G - 1):
+            load_words(3, g, g + 1, 0, H)
         for s in range(LAST_SPLIT):
             w = H // LAST_SPLIT
             load_words(3, G - 1, G, s * w, (s + 1) * w)

@@ -114,11 +114,11 @@ def tile_batchedlstm_w_kernel(
             load_words(2, g, g + 2, 0, H)
         load_words(3, 0, 2, 0, H)
         load_words(3, 2, 4, 0, H)
-        for g in range(4, G - 1):
+        for g in range(4, G - 2):
             load_words(3, g, g + 1, 0, H)
         for s in range(LAST_SPLIT):
             w = H // LAST_SPLIT
-            load_words(3, G - 1, G, s * w, (s + 1) * w)
+            load_words(3, G - 2, G, s * w, (s + 1) * w)
 
         x_words = x_sb[:].bitcast(F32)
         for g in range(GX):
@@ -202,8 +202,12 @@ def tile_batchedlstm_w_kernel(
             nc.sync.dma_start(out=out_2[b].rearrange("(c p) f -> p c f", p=P),
                               in_=nc_sb[:, :, b * F:(b + 1) * F])
 
-        for g in range(G):
+        for g in range(G - 2):
             passes(3, g, allc)
+        for s in range(LAST_SPLIT):
+            pair = [2 * s, 2 * s + 1]
+            passes(3, G - 2, pair)
+            passes(3, G - 1, pair)
         activate(3, allc)
 
         out_0_rows = out_0.rearrange("b f h -> (b f) h")

from contextlib import ExitStack

import concourse.mybir as mybir
from concourse.masks import make_identity

F32 = mybir.dt.float32
BF16 = mybir.dt.bfloat16
I32 = mybir.dt.int32
U32 = mybir.dt.uint32
U8 = mybir.dt.uint8
FP8X4 = mybir.dt.float8_e4m3fn_x4
ACT = mybir.ActivationFunctionType
ALU = mybir.AluOpType

P = 128
B, F, C, H = 2, 64, 3072, 1024
K = C + H
G = K // 512
GX = C // 512
NCH = H // P
FLOPS = 2 * 4 * H * K * B * F
LAST_SPLIT = 4
SCALES_ON_SYNC = [0]


def tile_batchedlstm_w_kernel(
    tc, x, hidden_state, cell_state,
    W_f_words, W_f_scales, b_f,
    W_i_words, W_i_scales, b_i,
    W_o_words, W_o_scales, b_o,
    W_g_words, W_g_scales, b_g,
    out_0, out_1, out_2,
):
    nc = tc.nc
    words = [W_f_words, W_i_words, W_g_words, W_o_words]
    scales = [W_f_scales, W_i_scales, W_g_scales, W_o_scales]
    biases = [b_f, b_i, b_g, b_o]
    funcs = [ACT.Sigmoid, ACT.Sigmoid, ACT.Tanh, ACT.Sigmoid]

    with ExitStack() as ctx:
        keep = ctx.enter_context(tc.tile_pool(name="keep", bufs=1))
        psum = ctx.enter_context(tc.psum_pool(name="psum", bufs=1))
        ctx.enter_context(tc.manual_schedule())

        w_sb = [keep.tile([P, G, H], U32, name="w%d" % gi, align_bytes=64) for gi in range(4)]
        planes = keep.tile([P, 4, 2, H], U8, name="planes", align_bytes=64)
        x_sb = keep.tile([P, C], BF16, name="x_sb", align_bytes=64)
        h_raw = keep.tile([P, 2, B, 4 * F], BF16, name="h_raw", align_bytes=64)
        grouped = keep.tile([P, G, P, 4], BF16, name="grouped", align_bytes=64)
        xh_codes = keep.tile([P, G, P], U32, name="xh_codes", align_bytes=64)
        xh_scales = keep.tile([P, G, P], U8, name="xh_scales", align_bytes=64)
        ident = keep.tile([P, P], F32, name="ident")
        b_raw = keep.tile([P, P], BF16, name="b_raw")
        b_f32 = keep.tile([P, P], F32, name="b_f32")
        bias_sb = keep.tile([P, 32], F32, name="bias_sb")
        ident_bf = keep.tile([P, P], BF16, name="ident_bf")
        c_raw = keep.tile([P, B, NCH, F], BF16, name="c_raw")
        c_byj = keep.tile([P, NCH, P], BF16, name="c_byj")
        c_tok = keep.tile([P, H], BF16, name="c_tok")
        c_sb = keep.tile([P, NCH, P], BF16, name="c_sb")
        gate_sb = [keep.tile([P, NCH, P], F32, name="gate%d" % gi) for gi in range(4)]
        nc_sb = keep.tile([P, NCH, P], F32, name="nc_sb")
        th_sb = keep.tile([P, NCH, P], F32, name="th_sb")
        nh_sb = keep.tile([P, NCH, P], F32, name="nh_sb")
        o0_sb = keep.tile([P, NCH, P], F32, name="o0_sb")
        bank = [psum.tile([P, 4, P], F32, name="bank%d" % j) for j in range(8)]

        nc.vector.memset(planes[:].rearrange("p a b n -> p (a b n)").bitcast(I32), 0)
        nc.vector.memset(b_raw[:], 0.0)
        make_identity(nc, ident[:])
        make_identity(nc, ident_bf[:])

        def load_bias(gi):
            nc.sync.dma_start(out=b_raw[8 * gi:8 * gi + 8, :],
                              in_=biases[gi].rearrange("(c p) -> c p", p=P))

        def load_scale(gi, j):
            gh, q = divmod(j, 4)
            dst = planes[32 * q:32 * q + 16, gi, gh, :]
            src = scales[gi][4 * gh:4 * gh + 4, 4 * q:4 * q + 4, :]
            if gi in SCALES_ON_SYNC:
                nc.sync.dma_start(out=dst.bitcast(I32), in_=src.bitcast(I32))
            else:
                nc.gpsimd.dma_start(out=dst.bitcast(F32), in_=src.bitcast(F32))

        def load_words(gi, g0, g1, n0, n1):
            nc.sync.dma_start(
                out=w_sb[gi][:, g0:g1, n0:n1].bitcast(I32),
                in_=words[gi][g0:g1].rearrange("g p n t -> p g (n t)")[:, :, 4 * n0:4 * n1].bitcast(I32))

        def load_hidden(b):
            nc.sync.dma_start(
                out=h_raw[:, :, b, :],
                in_=hidden_state[b].rearrange("(g p t) f -> p g (t f)", g=2, p=P, t=4))

        for gi in range(1, 4):
            for j in range(8):
                load_scale(gi, j)
        nc.sync.dma_start(out=x_sb[:], in_=x.rearrange("b f c -> (b f) c"))
        nc.sync.dma_start(out=c_raw[:].rearrange("p b j f -> p b (j f)"),
                          in_=cell_state.rearrange("b (p j) f -> p b (j f)", j=NCH))
        small = [lambda: load_scale(0, 0), lambda: load_scale(0, 1), lambda: load_scale(0, 2),
                 lambda: load_scale(0, 3), lambda: load_hidden(0), lambda: load_hidden(1),
                 lambda: load_scale(0, 4), lambda: load_scale(0, 5), lambda: load_scale(0, 6),
                 lambda: load_scale(0, 7), lambda: load_bias(0), lambda: load_bias(1),
                 lambda: load_bias(2), lambda: load_bias(3)]
        for g in range(0, G, 2):
            load_words(0, g, g + 2, 0, H)
            for issue in small[2 * g:2 * g + 4]:
                issue()
        for g in range(0, G, 4):
            load_words(1, g, g + 4, 0, H)
        for g in range(0, G, 2):
            load_words(2, g, g + 2, 0, H)
        load_words(3, 0, 2, 0, H)
        load_words(3, 2, 4, 0, H)
        for g in range(4, G - 2):
            load_words(3, g, g + 1, 0, H)
        for s in range(LAST_SPLIT):
            w = H // LAST_SPLIT
            load_words(3, G - 2, G, s * w, (s + 1) * w)

        x_words = x_sb[:].bitcast(F32)
        for g in range(GX):
            for u in range(2):
                nc.tensor.transpose(bank[g // 2][:, (g % 2) * 2 + u, :],
                                    x_words[:, 256 * g + u:256 * (g + 1):2], ident[:])

        tok_bank = bank[4][:].rearrange("p a m -> p (a m)").bitcast(BF16)
        back_bank = bank[5][:].rearrange("p a m -> p (a m)").bitcast(BF16)
        nc.scalar.copy(out=c_byj[:].rearrange("p j (b f) -> p j b f", b=B),
                       in_=c_raw[:].rearrange("p b j f -> p j b f"))
        for j in range(NCH):
            nc.tensor.transpose(tok_bank[:, j * P:(j + 1) * P], c_byj[:, j, :], ident_bf[:])

        grouped_w = grouped[:].bitcast(F32)

        def x_src(j):
            return bank[j][:].rearrange("p (g u) c -> p g c u", u=2)

        def quantise(half):
            gs = slice(4 * half, 4 * half + 4)
            nc.vector.quantize_mx(
                out=xh_codes[:, gs, :].rearrange("p g c -> p (g c)").bitcast(FP8X4),
                scales=xh_scales[:, gs, :].rearrange("p g c -> p (g c)"),
                in_=grouped[:, gs, :, :].rearrange("p g c t -> p (g c t)"))

        nc.vector.tensor_copy(out=grouped_w[:, 0:2, :, :], in_=x_src(0))
        nc.scalar.copy(out=grouped_w[:, 2:4, :, :], in_=x_src(1))
        nc.scalar.copy(out=c_tok[:].rearrange("t (p j) -> t p j", j=NCH),
                       in_=tok_bank.rearrange("t (j p) -> t p j", j=NCH))
        for hc in range(NCH):
            nc.tensor.transpose(back_bank[:, hc * P:(hc + 1) * P], c_tok[:, hc * P:(hc + 1) * P], ident_bf[:])
        nc.scalar.copy(out=c_sb[:].rearrange("p c m -> p (c m)"), in_=back_bank)
        nc.vector.tensor_copy(out=grouped_w[:, 4:6, :, :], in_=x_src(2))
        quantise(0)
        nc.vector.tensor_copy(
            out=grouped[:, GX:G, :, :].rearrange("p g (b f) t -> p (g b) f t", b=B),
            in_=h_raw[:].rearrange("p g b (t f) -> p (g b) f t", t=4))
        quantise(1)
        nc.vector.tensor_copy(out=b_f32[:], in_=b_raw[:])

        def passes(gi, g, chunks):
            k = 4 * (g % 4)
            for hc in chunks:
                cols = slice(hc * P, (hc + 1) * P)
                nc.tensor.matmul_mx(
                    out=bank[hc][:, gi, :],
                    lhsT=w_sb[gi][:, g, cols].bitcast(FP8X4),
                    lhsT_scale=planes[k:P, gi, g // 4, cols],
                    rhs=xh_codes[:, g, :].bitcast(FP8X4),
                    rhs_scale=xh_scales[:, g, :],
                    start=(g == 0), stop=(g == G - 1))

        def activate(gi, chunks):
            for hc in chunks:
                nc.scalar.activation(
                    out=gate_sb[gi][:, hc, :], in_=bank[hc][:, gi, :], func=funcs[gi],
                    bias=bias_sb[:, 8 * gi + hc:8 * gi + hc + 1], scale=1.0)

        allc = list(range(NCH))
        for g in range(G):
            passes(0, g, allc)
        nc.tensor.transpose(bank[3][:, 3, :], b_f32[:], ident[:])
        nc.vector.tensor_copy(out=bias_sb[:], in_=bank[3][:, 3, 0:32])
        activate(0, allc)
        nc.vector.tensor_tensor(out=gate_sb[0][:], in0=gate_sb[0][:], in1=c_sb[:], op=ALU.mult)
        for g in range(G):
            passes(1, g, allc)
        activate(1, allc)
        for g in range(G):
            passes(2, g, allc)
        activate(2, allc)
        for half in range(2):
            hs = slice(4 * half, 4 * half + 4)
            nc.vector.tensor_tensor(out=gate_sb[1][:, hs, :], in0=gate_sb[1][:, hs, :],
                                    in1=gate_sb[2][:, hs, :], op=ALU.mult)
            nc.vector.tensor_tensor(out=nc_sb[:, hs, :], in0=gate_sb[0][:, hs, :],
                                    in1=gate_sb[1][:, hs, :], op=ALU.add)
            nc.scalar.activation(out=th_sb[:, hs, :], in_=nc_sb[:, hs, :], func=ACT.Tanh)
        for b in range(B):
            nc.sync.dma_start(out=out_2[b].rearrange("(c p) f -> p c f", p=P),
                              in_=nc_sb[:, :, b * F:(b + 1) * F])

        for g in range(G - 2):
            passes(3, g, allc)
        for s in range(LAST_SPLIT):
            pair = [2 * s, 2 * s + 1]
            passes(3, G - 2, pair)
            passes(3, G - 1, pair)
        activate(3, allc)

        out_0_rows = out_0.rearrange("b f h -> (b f) h")

        def product(j):
            cs = slice(2 * j, 2 * j + 2)
            nc.vector.tensor_tensor(out=nh_sb[:, cs, :], in0=th_sb[:, cs, :],
                                    in1=gate_sb[3][:, cs, :], op=ALU.mult)
            for u in range(2):
                nc.tensor.transpose(bank[2 * j][:, u, :], nh_sb[:, 2 * j + u, :], ident[:])

        def store_hidden(q):
            cs = slice(4 * q, 4 * q + 4)
            for b in range(B):
                nc.sync.dma_start(
                    out=out_1[b].rearrange("(c p) f -> p c f", p=P)[:, cs, :],
                    in_=nh_sb[:, cs, b * F:(b + 1) * F])

        def leave(j, eng_copy):
            cs = slice(2 * j, 2 * j + 2)
            eng_copy(out=o0_sb[:, cs, :], in_=bank[2 * j][:, 0:2, :])

        def store_tokens(q):
            cs = slice(4 * q, 4 * q + 4)
            nc.sync.dma_start(out=out_0_rows[:, 4 * q * P:(4 * q + 4) * P],
                              in_=o0_sb[:, cs, :].rearrange("p c m -> p (c m)"))

        product(0)
        product(1)
        store_hidden(0)
        leave(0, nc.vector.tensor_copy)
        product(2)
        leave(1, nc.vector.tensor_copy)
        store_tokens(0)
        product(3)
        store_hidden(1)
        leave(2, nc.scalar.copy)
        leave(3, nc.scalar.copy)
        store_tokens(1)
